import numpy as np
import ml_dtypes


def mxq(x, axis, fmt="e4m3"):
    dtype, down = {"e4m3": (ml_dtypes.float8_e4m3fn, 7), "e5m2": (ml_dtypes.float8_e5m2, 14)}[fmt]
    v = np.moveaxis(np.asarray(x, np.float32).astype(ml_dtypes.bfloat16).astype(np.float64), axis, -1)
    blocks = v.reshape(v.shape[:-1] + (-1, 32))
    amax = np.abs(blocks).max(-1, keepdims=True)
    byte = np.maximum(np.where(amax > 0, np.frexp(amax)[1] - 1 + 127, 0) - down, 1)
    scale = np.exp2(byte - 127.0)
    codes = (blocks / scale).astype(np.float32).astype(dtype).astype(np.float64)
    return np.moveaxis((codes * scale).reshape(v.shape), -1, axis)


WIDE = False


def mx_kscale(k):
    if not WIDE:
        return np.ones(k)
    levels = np.array([10, -10, 5, -5, 0])
    a = np.random.permutation(np.resize(levels, k // 512 * 4)).reshape(k // 512, 4)
    idx = np.arange(k)
    return np.exp2(a[idx // 512, idx % 128 // 32])


BF16 = ml_dtypes.bfloat16


def bf(x):
    return np.asarray(x, np.float32).astype(BF16)


def f64(x):
    return np.asarray(x).astype(np.float64)


B, S, D, DK, H = 2, 512, 1024, 1024, 8
DH = D // H
LN_EPS = 1e-8


def split_heads(x):
    return x.reshape(B, S, H, DH).transpose(0, 2, 1, 3).reshape(B * H, S, DH)


def merge_heads(x):
    return x.reshape(B, H, S, DH).transpose(0, 2, 1, 3).reshape(B, S, D)


def setup_inputs():
    s = mx_kscale(DK)
    keep = np.random.random((B, S, 1)) > 0.25
    return {"q_relu": bf(np.maximum(np.random.standard_normal((B, S, D)) * 2.2, 0.0)),
            "k_relu": bf(np.maximum(np.random.standard_normal((B, S, D)) * 2.2, 0.0)),
            "keys": bf(np.random.standard_normal((B, S, DK)) * s),
            "Wv": bf(np.random.standard_normal((D, DK)) * 2.2 / np.sqrt(DK) / s[None, :]),
            "bv": bf(np.random.standard_normal(D) * 0.3),
            "queries": bf(np.random.standard_normal((B, S, D)) * keep),
            "ln_gamma": bf(1.0 + 0.1 * np.random.standard_normal(D)),
            "ln_beta": bf(0.1 * np.random.standard_normal(D))}


def reference(q_relu, k_relu, keys, Wv, bv, queries, ln_gamma, ln_beta):
    x = f64(queries)
    v = np.maximum((mxq(f64(keys), 2, "e4m3") @ mxq(f64(Wv), 1, "e4m3").T) + f64(bv), 0.0)
    q_, k_, v_ = split_heads(f64(q_relu)), split_heads(f64(k_relu)), split_heads(v)
    sc = q_ @ k_.transpose(0, 2, 1) / np.sqrt(DH)
    e = np.exp(sc - sc.max(-1, keepdims=True))
    mask = np.tile(np.where(np.abs(x).sum(-1, keepdims=True) > 0, 1.0, 0.0), (H, 1, 1))
    o = (mxq(e, 2, "e4m3") @ mxq(v_, 1, "e4m3")) / e.sum(-1, keepdims=True) * mask
    y = merge_heads(o) + x
    mu = y.mean(-1, keepdims=True)
    var = np.square(y - mu).mean(-1, keepdims=True)
    return (y - mu) / np.sqrt(var + LN_EPS) * f64(ln_gamma) + f64(ln_beta)

@@ -1,0 +1,537 @@
+import math
+from contextlib import ExitStack
+
+import concourse.mybir as mybir
+from concourse.masks import make_identity
+
+F32 = mybir.dt.float32
+BF16 = mybir.dt.bfloat16
+U32 = mybir.dt.uint32
+U8 = mybir.dt.uint8
+FP8X4 = mybir.dt.float8_e4m3fn_x4
+ACT = mybir.ActivationFunctionType
+ALU = mybir.AluOpType
+
+P = 128
+B = 2
+S = 512
+D = 1024
+H = 8
+DH = D // H
+TT = S // P
+SCALE = 1.0 / math.sqrt(DH)
+LN_EPS = 1e-8
+
+UNITS = B * TT
+HALVES = UNITS * 2
+PAIRS = UNITS * 4
+JOBS_PER_STEP = 2
+AHEAD = 1
+SNEG_BUFS = 2 * AHEAD + 4
+VECTOR_UNITS = 2
+RELU_SPLIT = 4
+LEAD = 2
+
+FLOPS = 2 * B * S * D * D + 2 * 2 * B * H * S * S * DH
+
+
+def tile_multiheadattentionlayer_pa_kernel(
+    tc, q_relu, k_relu, keys, Wv, bv, queries, ln_gamma, ln_beta, out
+):
+    nc = tc.nc
+    with ExitStack() as ctx:
+        ctx.enter_context(tc.manual_schedule())
+        const = ctx.enter_context(tc.tile_pool(name="const", bufs=1))
+        keep = ctx.enter_context(tc.tile_pool(name="keep", bufs=1))
+        raw_pool = ctx.enter_context(tc.tile_pool(name="raw", bufs=8))
+        grp_pool = ctx.enter_context(tc.tile_pool(name="grp", bufs=2))
+        vt_pool = ctx.enter_context(tc.tile_pool(name="vt", bufs=3))
+        s_pool = ctx.enter_context(tc.tile_pool(name="s", bufs=SNEG_BUFS))
+        e_pool = ctx.enter_context(tc.tile_pool(name="e", bufs=3))
+        eg_pool = ctx.enter_context(tc.tile_pool(name="eg", bufs=3))
+        ec_pool = ctx.enter_context(tc.tile_pool(name="ec", bufs=3))
+        y_pool = ctx.enter_context(tc.tile_pool(name="y", bufs=3))
+        junk_pool = ctx.enter_context(tc.tile_pool(name="junk", bufs=2))
+        small = ctx.enter_context(tc.tile_pool(name="small", bufs=4))
+        bank_psum = ctx.enter_context(tc.psum_pool(name="bank", bufs=5))
+        s_psum = ctx.enter_context(tc.psum_pool(name="sc", bufs=2))
+        o_psum = ctx.enter_context(tc.psum_pool(name="o", bufs=1))
+
+        ident_b = const.tile([P, P], BF16)
+        make_identity(nc, ident_b[:])
+        ident_w = const.tile([P, P], F32)
+        make_identity(nc, ident_w[:])
+        neg_half = const.tile([P, 1], F32)
+        nc.vector.memset(neg_half[:], -0.5)
+        warm = const.tile([P, 1], F32)
+        nc.scalar.activation(out=warm[:], in_=neg_half[:], func=ACT.Exp)
+        bv_rows = const.tile([P, P], BF16)
+        nc.vector.memset(bv_rows[:], 0.0)
+        nc.scalar.dma_start(out=bv_rows[0:H, :], in_=bv.rearrange("(t c) -> t c", c=P))
+
+        w_codes = keep.tile([P, 2048], U32, align_bytes=64)
+        w_scales = keep.tile([P, 2048], U8, align_bytes=64)
+        k_codes = keep.tile([P, 2048], U32, align_bytes=64)
+        k_scales = keep.tile([P, 2048], U8, align_bytes=64)
+        v_codes = keep.tile([P, 2048], U32, align_bytes=64)
+        v_scales = keep.tile([P, 2048], U8, align_bytes=64)
+        qT = keep.tile([P, B * H * S], BF16)
+        kT = keep.tile([P, B * H * S], BF16)
+        x_sb = keep.tile([P, B * TT * D], BF16)
+        gamma_b = keep.tile([P, D], BF16)
+        beta_b = keep.tile([P, D], BF16)
+        msk = keep.tile([P, TT * B], F32)
+        bvT = keep.tile([P, H], F32)
+        heads_T = {
+            "q": qT[:].rearrange("p (b h s) -> p b h s", b=B, h=H),
+            "k": kT[:].rearrange("p (b h s) -> p b h s", b=B, h=H),
+        }
+        x_v = x_sb[:].rearrange("p (t k) -> p t k", t=B * TT)
+
+        raws = {}
+
+        def load(key, rows):
+            raw = raw_pool.tile([P, 2 * D], BF16, tag="raw", name="raw")
+            nc.sync.dma_start(
+                out=raw[:].rearrange("p (a k) -> p a k", a=2),
+                in_=rows.rearrange("(a p) k -> p a k", p=P),
+            )
+            raws[key] = raw
+
+        def load_batch(name, src, b):
+            for a2 in range(2):
+                load((name, b, a2), src[b, a2 * 2 * P : (a2 + 1) * 2 * P, :])
+
+        load_batch("k", k_relu, 0)
+        load_batch("q", q_relu, 0)
+        load_batch("keys", keys, 0)
+        for a2 in range(4):
+            load(("w", 0, a2), Wv[a2 * 2 * P : (a2 + 1) * 2 * P, :])
+        for b in range(B):
+            nc.sync.dma_start(
+                out=x_v[:, b * TT : (b + 1) * TT, :],
+                in_=queries[b].rearrange("(t p) k -> p t k", p=P),
+            )
+        load_batch("keys", keys, 1)
+        nc.sync.dma_start(out=gamma_b[:], in_=ln_gamma.partition_broadcast(P))
+        nc.sync.dma_start(out=beta_b[:], in_=ln_beta.partition_broadcast(P))
+        load_batch("k", k_relu, 1)
+        load_batch("q", q_relu, 1)
+
+        tiles = {}
+        done = set()
+
+        def word_transposes(key, words):
+            bank = bank_psum.tile([P, 512], F32, tag="bank", name="bank")
+            for k in range(4):
+                cols = slice(k * P, (k + 1) * P)
+                nc.tensor.transpose(bank[:, cols], words[:, cols], ident_w[:])
+            tiles[key] = bank
+
+        def copy_interleaved(key, grouped, on_vector):
+            src = tiles[key][:].rearrange("p (a u r) -> p a r u", a=2, u=2)
+            if on_vector:
+                nc.vector.tensor_copy(out=grouped, in_=src)
+            else:
+                nc.scalar.copy(out=grouped, in_=src)
+
+        def as_blocks(words):
+            return words.rearrange("p (a r u) -> p a r u", a=2, u=2)
+
+        def heads_front(name, b, tt):
+            raw = raws[name, b, tt // 2]
+            bank = bank_psum.tile([P, 1024], BF16, tag="bank", name="bank_b")
+            for h in range(H):
+                first = (tt % 2) * D + h * DH
+                nc.tensor.transpose(
+                    bank[:, h * P : (h + 1) * P], raw[:, first : first + DH], ident_b[:]
+                )
+            tiles[name, b, tt] = bank
+
+        def heads_back(name, b, tt):
+            dst = heads_T[name][:, b, :, tt * P : (tt + 1) * P]
+            src = tiles[name, b, tt][:].rearrange("p (h r) -> p h r", h=H)
+            if name == "q":
+                nc.vector.tensor_copy(out=dst, in_=src)
+            else:
+                nc.scalar.copy(out=dst, in_=src)
+            done.add((name, b, tt))
+
+        def rows_front(name, b, t):
+            words = raws[name, b, t // 2][:].bitcast(F32)
+            word_transposes((name, b, t), words[:, (t % 2) * 512 : (t % 2 + 1) * 512])
+
+        def keys_back(name, b, tt):
+            if tt == 0:
+                tiles["kg", b] = grp_pool.tile([P, 4096], BF16, tag="grp", name="kg", align_bytes=64)
+            kg_v = tiles["kg", b][:].bitcast(F32).rearrange("p (g s u) -> p g s u", g=2, u=2)
+            copy_interleaved((name, b, tt), kg_v[:, :, tt * P : (tt + 1) * P, :], tt == TT - 1)
+
+        def quantise_keys(b):
+            cols = slice(b * 1024, (b + 1) * 1024)
+            nc.vector.quantize_mx(
+                out=k_codes[:, cols].bitcast(FP8X4), scales=k_scales[:, cols], in_=tiles["kg", b][:]
+            )
+            done.add(("keys", b))
+
+        def w_back(name, b, ct):
+            if ct % 4 == 0:
+                tiles["wg", ct // 4] = grp_pool.tile(
+                    [P, 4096], BF16, tag="grp", name="wg", align_bytes=64
+                )
+            wg_w = tiles["wg", ct // 4][:].bitcast(F32)
+            copy_interleaved(
+                (name, b, ct), as_blocks(wg_w[:, (ct % 4) * 512 : (ct % 4 + 1) * 512]), ct % 4 == 3
+            )
+
+        def quantise_w(half):
+            cols = slice(half * 1024, (half + 1) * 1024)
+            nc.vector.quantize_mx(
+                out=w_codes[:, cols].bitcast(FP8X4), scales=w_scales[:, cols], in_=tiles["wg", half][:]
+            )
+            done.add(("w", half))
+
+        def bias_front():
+            bv_bank = bank_psum.tile([P, 1024], BF16, tag="bank", name="bv_bank")
+            nc.tensor.transpose(bv_bank[:, 0:P], bv_rows[:], ident_b[:])
+            tiles["bv"] = bv_bank
+
+        def bias_back():
+            nc.vector.tensor_copy(out=bvT[:], in_=tiles["bv"][:, 0:H])
+
+        def project_front(b, h):
+            acc = bank_psum.tile([P, S], F32, tag="bank", name="acc")
+            for c in range(2):
+                wc = slice(h * 256 + c * P, h * 256 + (c + 1) * P)
+                kc = slice(b * 1024 + c * S, b * 1024 + (c + 1) * S)
+                nc.tensor.matmul_mx(
+                    out=acc[:],
+                    lhsT=w_codes[:, wc].bitcast(FP8X4),
+                    lhsT_scale=w_scales[:, wc],
+                    rhs=k_codes[:, kc].bitcast(FP8X4),
+                    rhs_scale=k_scales[:, kc],
+                    start=(c == 0),
+                    stop=(c == 1),
+                )
+            tiles["acc", b, h] = acc
+
+        def project_back(b, h):
+            if h % 2 == 0:
+                tiles["vT", b, h // 2] = vt_pool.tile([P, 2 * S], BF16, tag="vt", name="vT")
+            dst = tiles["vT", b, h // 2][:, (h % 2) * S : (h % 2 + 1) * S]
+            if h % RELU_SPLIT != RELU_SPLIT - 1:
+                nc.scalar.activation(
+                    out=dst, in_=tiles["acc", b, h][:], func=ACT.Relu, bias=bvT[:, h : h + 1], scale=1.0
+                )
+            else:
+                nc.vector.tensor_scalar(
+                    out=dst,
+                    in0=tiles["acc", b, h][:],
+                    scalar1=bvT[:, h : h + 1],
+                    scalar2=0.0,
+                    op0=ALU.add,
+                    op1=ALU.max,
+                )
+            done.add(("vT", b, h))
+
+        def v_front(b, g):
+            word_transposes(("vbank", b, g), tiles["vT", b, g][:].bitcast(F32))
+
+        def v_back(b, g):
+            if g % 2 == 0:
+                tiles["vg", b, g // 2] = eg_pool.tile(
+                    [P, 2048], BF16, tag="eg", name="vg", align_bytes=64
+                )
+            vg_w = tiles["vg", b, g // 2][:].bitcast(F32)
+            copy_interleaved(
+                ("vbank", b, g), as_blocks(vg_w[:, (g % 2) * 512 : (g % 2 + 1) * 512]), g % 2 == 1
+            )
+
+        def quantise_v(b, half):
+            cols = slice((b * 2 + half) * 512, (b * 2 + half + 1) * 512)
+            nc.vector.quantize_mx(
+                out=v_codes[:, cols].bitcast(FP8X4),
+                scales=v_scales[:, cols],
+                in_=tiles["vg", b, half][:],
+            )
+            done.add(("v", b, half))
+
+        def mask_rows(b, tt):
+            mjunk = junk_pool.tile([P, D], BF16, tag="mjunk", name="mjunk")
+            nc.vector.tensor_scalar(
+                out=mjunk[:],
+                in0=x_v[:, b * TT + tt, :],
+                scalar1=0.0,
+                scalar2=None,
+                op0=ALU.not_equal,
+                op1=ALU.max,
+                accum_out=msk[:, tt * B + b : tt * B + b + 1],
+            )
+            done.add(("mask", b, tt))
+
+        jobs = []
+        for b in range(B):
+            for name in ("k", "q"):
+                jobs.extend([(heads_front, heads_back, (name, b, tt), ()) for tt in range(TT)])
+            jobs.extend([(rows_front, keys_back, ("keys", b, tt), ()) for tt in range(TT)])
+            jobs.append((None, quantise_keys, (b,), ()))
+            if b == 0:
+                jobs.append((bias_front, bias_back, (), ()))
+                for half in range(2):
+                    jobs.extend(
+                        [(rows_front, w_back, ("w", 0, half * 4 + c4), ()) for c4 in range(4)]
+                    )
+                    jobs.append((None, quantise_w, (half,), ()))
+                jobs.extend([(None, mask_rows, (bb, 0), ()) for bb in range(B)])
+            jobs.extend(
+                [
+                    (project_front, project_back, (b, h), (("keys", b), ("w", h // 4)))
+                    for h in range(H)
+                ]
+            )
+            jobs.extend([(v_front, v_back, (b, g), (("vT", b, 2 * g + 1),)) for g in range(4)])
+            jobs.extend([(None, quantise_v, (b, half), ()) for half in range(2)])
+            if b == 0:
+                for tt in range(1, TT):
+                    jobs.extend([(None, mask_rows, (bb, tt), ()) for bb in range(B)])
+        issued = {"front": 0, "back": 0}
+
+        def advance():
+            if issued["back"] == len(jobs):
+                return
+            while issued["front"] < min(issued["back"] + LEAD + 1, len(jobs)):
+                front, back, args, before = jobs[issued["front"]]
+                if not all(key in done for key in before):
+                    break
+                if front is not None:
+                    front(*args)
+                issued["front"] += 1
+            front, back, args, before = jobs[issued["back"]]
+            back(*args)
+            issued["back"] += 1
+
+        def need(key):
+            while key not in done:
+                advance()
+
+        def scores(j):
+            for k in (2 * j, 2 * j + 1):
+                b, it, h = k // (H * TT), (k // H) % TT, k % H
+                need(("k", b, TT - 1))
+                need(("q", b, it))
+                s_bank = s_psum.tile([P, S], F32, tag="s", name="s_bank")
+                nc.tensor.matmul(
+                    out=s_bank[:],
+                    lhsT=heads_T["q"][:, b, h, it * P : (it + 1) * P],
+                    rhs=heads_T["k"][:, b, h, :],
+                    start=True,
+                    stop=True,
+                )
+                tiles["s", k] = s_bank
+
+        def row_max(j):
+            for k in (2 * j, 2 * j + 1):
+                sneg = s_pool.tile([P, S], F32, tag="sneg", name="sneg")
+                nbias = small.tile([P, 1], F32, tag="nbias", name="nbias", bufs=SNEG_BUFS)
+                nc.vector.tensor_scalar(
+                    out=sneg[:],
+                    in0=tiles["s", k][:],
+                    scalar1=-SCALE,
+                    scalar2=None,
+                    op0=ALU.mult,
+                    op1=ALU.min,
+                    accum_out=nbias[:],
+                )
+                tiles["sneg", k] = sneg
+                tiles["nbias", k] = nbias
+
+        def exponentials(j):
+            if j % 2 == 0:
+                tiles["rowsum", j // 2] = small.tile([P, 4], F32, tag="rowsum", name="rowsum")
+            e2 = e_pool.tile([P, 2 * S], BF16, tag="e", name="e2")
+            for hh in range(2):
+                k = 2 * j + hh
+                nc.scalar.activation(
+                    out=e2[:, hh * S : (hh + 1) * S],
+                    in_=tiles["sneg", k][:],
+                    func=ACT.Exp,
+                    bias=tiles["nbias", k][:],
+                    scale=-1.0,
+                    accum_out=tiles["rowsum", j // 2][:, k % 4 : k % 4 + 1],
+                )
+            tiles["e", j] = e2
+
+        def transpose_e(j):
+            word_transposes(("ebank", j), tiles["e", j][:].bitcast(F32))
+
+        def copy_e(j):
+            if j % 2 == 0:
+                tiles["eg", j // 2] = eg_pool.tile(
+                    [P, 2048], BF16, tag="eg", name="eg", align_bytes=64
+                )
+            eg_w = tiles["eg", j // 2][:].bitcast(F32)
+            copy_interleaved(
+                ("ebank", j), as_blocks(eg_w[:, (j % 2) * 512 : (j % 2 + 1) * 512]), False
+            )
+
+        def quantise_e(n):
+            it = (n // 2) % TT
+            need(("mask", 0, it))
+            need(("mask", 1, it))
+            rinv = small.tile([P, 4], F32, tag="rinv", name="rinv")
+            nc.vector.reciprocal(out=rinv[:], in_=tiles["rowsum", n][:])
+            r = small.tile([P, 4], F32, tag="r", name="r")
+            nc.vector.tensor_tensor(
+                out=r[:].rearrange("p (a c) -> p a c", a=2),
+                in0=rinv[:].rearrange("p (a c) -> p a c", a=2),
+                in1=msk[:, it * B : (it + 1) * B].unsqueeze(1).to_broadcast([P, 2, B]),
+                op=ALU.mult,
+            )
+            tiles["r", n] = r
+            e_codes = ec_pool.tile([P, 512], U32, tag="ec", name="e_codes", align_bytes=64)
+            e_scales = ec_pool.tile([P, 512], U8, tag="es", name="e_scales", align_bytes=64)
+            nc.vector.quantize_mx(
+                out=e_codes[:].bitcast(FP8X4), scales=e_scales[:], in_=tiles["eg", n][:]
+            )
+            tiles["ec", n] = e_codes
+            tiles["es", n] = e_scales
+
+        def e_times_v(n):
+            b = n // (2 * TT)
+            need(("v", b, n % 2))
+            o_bank = o_psum.tile([P, 512], F32, tag="o", name="o_bank")
+            for h4 in range(4):
+                h = (n % 2) * 4 + h4
+                ec = slice(h4 * P, (h4 + 1) * P)
+                vc = slice((b * H + h) * P, (b * H + h + 1) * P)
+                nc.tensor.matmul_mx(
+                    out=o_bank[:, ec],
+                    lhsT=tiles["ec", n][:, ec].bitcast(FP8X4),
+                    lhsT_scale=tiles["es", n][:, ec],
+                    rhs=v_codes[:, vc].bitcast(FP8X4),
+                    rhs_scale=v_scales[:, vc],
+                    start=True,
+                    stop=True,
+                )
+            tiles["o", n] = o_bank
+
+        def residual(n):
+            m = n // 2
+            if n % 2 == 0:
+                tiles["y", m] = y_pool.tile([P, D], F32, tag="y", name="y")
+                tiles["ysum", m] = small.tile([P, H], F32, tag="ysum", name="ysum")
+            for h4 in range(4):
+                h = (n % 2) * 4 + h4
+                nc.vector.scalar_tensor_tensor(
+                    out=tiles["y", m][:, h * DH : (h + 1) * DH],
+                    in0=tiles["o", n][:, h4 * P : (h4 + 1) * P],
+                    scalar=tiles["r", n][:, h4 : h4 + 1],
+                    in1=x_v[:, m, h * DH : (h + 1) * DH],
+                    op0=ALU.mult,
+                    op1=ALU.add,
+                    accum_out=tiles["ysum", m][:, h : h + 1],
+                )
+            if n % 2 == 1:
+                junk8 = small.tile([P, H], F32, tag="junk8", name="junk8")
+                negmu = small.tile([P, 1], F32, tag="negmu", name="negmu")
+                nc.vector.tensor_scalar(
+                    out=junk8[:],
+                    in0=tiles["ysum", m][:],
+                    scalar1=-1.0 / D,
+                    scalar2=None,
+                    op0=ALU.mult,
+                    op1=ALU.add,
+                    accum_out=negmu[:],
+                )
+                tiles["negmu", m] = negmu
+
+        def row_statistics(m):
+            sq = junk_pool.tile([P, D], BF16, tag="sq", name="sq")
+            ssq = small.tile([P, 1], F32, tag="ssq", name="ssq")
+            nc.scalar.activation(
+                out=sq[:],
+                in_=tiles["y", m][:],
+                func=ACT.Square,
+                bias=tiles["negmu", m][:],
+                scale=1.0,
+                accum_out=ssq[:],
+            )
+            veps = small.tile([P, 1], F32, tag="veps", name="veps")
+            nc.gpsimd.tensor_scalar(
+                out=veps[:], in0=ssq[:], scalar1=1.0 / D, scalar2=LN_EPS, op0=ALU.mult, op1=ALU.add
+            )
+            rstd = small.tile([P, 1], F32, tag="rstd", name="rstd")
+            nc.gpsimd.tensor_tensor(out=rstd[:], in0=veps[:], in1=neg_half[:], op=ALU.pow)
+            tiles["rstd", m] = rstd
+
+        def normalise(m):
+            y = tiles["y", m]
+            negmu = tiles["negmu", m]
+            rstd = tiles["rstd", m]
+            res = y_pool.tile([P, D], F32, tag="res", name="res")
+            rows = out[m // TT, (m % TT) * P : (m % TT + 1) * P, :]
+            halves = (slice(0, 512), slice(512, 1024))
+            if m < UNITS - VECTOR_UNITS:
+                for cols in halves:
+                    nc.gpsimd.tensor_scalar(
+                        out=res[:, cols],
+                        in0=y[:, cols],
+                        scalar1=negmu[:],
+                        scalar2=rstd[:],
+                        op0=ALU.add,
+                        op1=ALU.mult,
+                    )
+                    nc.gpsimd.tensor_tensor(
+                        out=res[:, cols], in0=res[:, cols], in1=gamma_b[:, cols], op=ALU.mult
+                    )
+                    nc.gpsimd.tensor_tensor(
+                        out=res[:, cols], in0=res[:, cols], in1=beta_b[:, cols], op=ALU.add
+                    )
+                    nc.sync.dma_start(out=rows[:, cols], in_=res[:, cols])
+            else:
+                for cols in halves:
+                    nc.vector.scalar_tensor_tensor(
+                        out=res[:, cols],
+                        in0=y[:, cols],
+                        scalar=negmu[:],
+                        in1=gamma_b[:, cols],
+                        op0=ALU.add,
+                        op1=ALU.mult,
+                    )
+                for cols in halves:
+                    nc.vector.scalar_tensor_tensor(
+                        out=res[:, cols],
+                        in0=res[:, cols],
+                        scalar=rstd[:],
+                        in1=beta_b[:, cols],
+                        op0=ALU.mult,
+                        op1=ALU.add,
+                    )
+                    nc.sync.dma_start(out=rows[:, cols], in_=res[:, cols])
+
+        for j in range(AHEAD):
+            scores(j)
+            row_max(j)
+        scores(AHEAD)
+        for step in range(PAIRS + 5):
+            if 0 <= step - 1 < PAIRS:
+                transpose_e(step - 1)
+            if step + AHEAD + 1 < PAIRS:
+                scores(step + AHEAD + 1)
+            if step + AHEAD < PAIRS:
+                row_max(step + AHEAD)
+            if step < PAIRS:
+                exponentials(step)
+            if 0 <= step - 1 < PAIRS:
+                copy_e(step - 1)
+            if step >= 3 and step % 2 == 1 and (step - 3) // 2 < HALVES:
+                quantise_e((step - 3) // 2)
+                e_times_v((step - 3) // 2)
+            if step >= 4 and step % 2 == 0 and (step - 4) // 2 < HALVES:
+                residual((step - 4) // 2)
+            if step >= 7 and step % 4 == 3:
+                row_statistics((step - 7) // 4)
+            if step >= 8 and step % 4 == 0:
+                normalise((step - 8) // 4)
+            for i in range(JOBS_PER_STEP):
+                advance()

@@ -26,6 +26,9 @@ UNITS = B * TT
 HALVES = UNITS * 2
 PAIRS = UNITS * 4
 JOBS_PER_STEP = 2
+EV_FIRST = 7
+EV_SECOND = 21
+JOBS_FIRST = 5
 AHEAD = 1
 SNEG_BUFS = 2 * AHEAD + 4
 VECTOR_UNITS = 2
@@ -49,10 +52,10 @@ def tile_multiheadattentionlayer_pa_kernel(
         s_pool = ctx.enter_context(tc.tile_pool(name="s", bufs=SNEG_BUFS))
         e_pool = ctx.enter_context(tc.tile_pool(name="e", bufs=3))
         eg_pool = ctx.enter_context(tc.tile_pool(name="eg", bufs=3))
-        ec_pool = ctx.enter_context(tc.tile_pool(name="ec", bufs=3))
+        ec_pool = ctx.enter_context(tc.tile_pool(name="ec", bufs=6))
         y_pool = ctx.enter_context(tc.tile_pool(name="y", bufs=3))
         junk_pool = ctx.enter_context(tc.tile_pool(name="junk", bufs=2))
-        small = ctx.enter_context(tc.tile_pool(name="small", bufs=4))
+        small = ctx.enter_context(tc.tile_pool(name="small", bufs=8))
         bank_psum = ctx.enter_context(tc.psum_pool(name="bank", bufs=5))
         s_psum = ctx.enter_context(tc.psum_pool(name="sc", bufs=2))
         o_psum = ctx.enter_context(tc.psum_pool(name="o", bufs=1))
@@ -165,14 +168,17 @@ def tile_multiheadattentionlayer_pa_kernel(
             if tt == 0:
                 tiles["kg", b] = grp_pool.tile([P, 4096], BF16, tag="grp", name="kg", align_bytes=64)
             kg_v = tiles["kg", b][:].bitcast(F32).rearrange("p (g s u) -> p g s u", g=2, u=2)
-            copy_interleaved((name, b, tt), kg_v[:, :, tt * P : (tt + 1) * P, :], tt == TT - 1)
+            copy_interleaved((name, b, tt), kg_v[:, :, tt * P : (tt + 1) * P, :], tt == TT - 3)
 
-        def quantise_keys(b):
-            cols = slice(b * 1024, (b + 1) * 1024)
+        def quantise_keys(b, c):
+            cols = slice(b * 1024 + c * S, b * 1024 + (c + 1) * S)
             nc.vector.quantize_mx(
-                out=k_codes[:, cols].bitcast(FP8X4), scales=k_scales[:, cols], in_=tiles["kg", b][:]
+                out=k_codes[:, cols].bitcast(FP8X4),
+                scales=k_scales[:, cols],
+                in_=tiles["kg", b][:, c * 2048 : (c + 1) * 2048],
             )
-            done.add(("keys", b))
+            if c == 1:
+                done.add(("keys", b))
 
         def w_back(name, b, ct):
             if ct % 4 == 0:
@@ -181,7 +187,7 @@ def tile_multiheadattentionlayer_pa_kernel(
                 )
             wg_w = tiles["wg", ct // 4][:].bitcast(F32)
             copy_interleaved(
-                (name, b, ct), as_blocks(wg_w[:, (ct % 4) * 512 : (ct % 4 + 1) * 512]), ct % 4 == 3
+                (name, b, ct), as_blocks(wg_w[:, (ct % 4) * 512 : (ct % 4 + 1) * 512]), ct % 4 == 1
             )
 
         def quantise_w(half):
@@ -244,7 +250,7 @@ def tile_multiheadattentionlayer_pa_kernel(
                 )
             vg_w = tiles["vg", b, g // 2][:].bitcast(F32)
             copy_interleaved(
-                ("vbank", b, g), as_blocks(vg_w[:, (g % 2) * 512 : (g % 2 + 1) * 512]), g % 2 == 1
+                ("vbank", b, g), as_blocks(vg_w[:, (g % 2) * 512 : (g % 2 + 1) * 512]), g % 2 == 0
             )
 
         def quantise_v(b, half):
@@ -274,7 +280,7 @@ def tile_multiheadattentionlayer_pa_kernel(
             for name in ("k", "q"):
                 jobs.extend([(heads_front, heads_back, (name, b, tt), ()) for tt in range(TT)])
             jobs.extend([(rows_front, keys_back, ("keys", b, tt), ()) for tt in range(TT)])
-            jobs.append((None, quantise_keys, (b,), ()))
+            jobs.extend([(None, quantise_keys, (b, c), ()) for c in range(2)])
             if b == 0:
                 jobs.append((bias_front, bias_back, (), ()))
                 for half in range(2):
@@ -381,6 +387,11 @@ def tile_multiheadattentionlayer_pa_kernel(
             rinv = small.tile([P, 4], F32, tag="rinv", name="rinv")
             nc.vector.reciprocal(out=rinv[:], in_=tiles["rowsum", n][:])
             r = small.tile([P, 4], F32, tag="r", name="r")
+            e_codes = ec_pool.tile([P, 512], U32, tag="ec", name="e_codes", align_bytes=64)
+            e_scales = ec_pool.tile([P, 512], U8, tag="es", name="e_scales", align_bytes=64)
+            nc.vector.quantize_mx(
+                out=e_codes[:].bitcast(FP8X4), scales=e_scales[:], in_=tiles["eg", n][:]
+            )
             nc.vector.tensor_tensor(
                 out=r[:].rearrange("p (a c) -> p a c", a=2),
                 in0=rinv[:].rearrange("p (a c) -> p a c", a=2),
@@ -388,11 +399,6 @@ def tile_multiheadattentionlayer_pa_kernel(
                 op=ALU.mult,
             )
             tiles["r", n] = r
-            e_codes = ec_pool.tile([P, 512], U32, tag="ec", name="e_codes", align_bytes=64)
-            e_scales = ec_pool.tile([P, 512], U8, tag="es", name="e_scales", align_bytes=64)
-            nc.vector.quantize_mx(
-                out=e_codes[:].bitcast(FP8X4), scales=e_scales[:], in_=tiles["eg", n][:]
-            )
             tiles["ec", n] = e_codes
             tiles["es", n] = e_scales
 
@@ -431,19 +437,19 @@ def tile_multiheadattentionlayer_pa_kernel(
                     op1=ALU.add,
                     accum_out=tiles["ysum", m][:, h : h + 1],
                 )
-            if n % 2 == 1:
-                junk8 = small.tile([P, H], F32, tag="junk8", name="junk8")
-                negmu = small.tile([P, 1], F32, tag="negmu", name="negmu")
-                nc.vector.tensor_scalar(
-                    out=junk8[:],
-                    in0=tiles["ysum", m][:],
-                    scalar1=-1.0 / D,
-                    scalar2=None,
-                    op0=ALU.mult,
-                    op1=ALU.add,
-                    accum_out=negmu[:],
-                )
-                tiles["negmu", m] = negmu
+        def mean(m):
+            junk8 = small.tile([P, H], F32, tag="junk8", name="junk8")
+            negmu = small.tile([P, 1], F32, tag="negmu", name="negmu")
+            nc.vector.tensor_scalar(
+                out=junk8[:],
+                in0=tiles["ysum", m][:],
+                scalar1=-1.0 / D,
+                scalar2=None,
+                op0=ALU.mult,
+                op1=ALU.add,
+                accum_out=negmu[:],
+            )
+            tiles["negmu", m] = negmu
 
         def row_statistics(m):
             sq = junk_pool.tile([P, D], BF16, tag="sq", name="sq")
@@ -456,64 +462,121 @@ def tile_multiheadattentionlayer_pa_kernel(
                 scale=1.0,
                 accum_out=ssq[:],
             )
+            inverse_deviation(m, ssq[:], 1.0 / D)
+
+        def inverse_deviation(m, squares, factor):
             veps = small.tile([P, 1], F32, tag="veps", name="veps")
             nc.gpsimd.tensor_scalar(
-                out=veps[:], in0=ssq[:], scalar1=1.0 / D, scalar2=LN_EPS, op0=ALU.mult, op1=ALU.add
+                out=veps[:], in0=squares, scalar1=factor, scalar2=LN_EPS, op0=ALU.mult, op1=ALU.add
             )
             rstd = small.tile([P, 1], F32, tag="rstd", name="rstd")
             nc.gpsimd.tensor_tensor(out=rstd[:], in0=veps[:], in1=neg_half[:], op=ALU.pow)
             tiles["rstd", m] = rstd
 
-        def normalise(m):
-            y = tiles["y", m]
-            negmu = tiles["negmu", m]
-            rstd = tiles["rstd", m]
-            res = y_pool.tile([P, D], F32, tag="res", name="res")
-            rows = out[m // TT, (m % TT) * P : (m % TT + 1) * P, :]
-            halves = (slice(0, 512), slice(512, 1024))
-            if m < UNITS - VECTOR_UNITS:
-                for cols in halves:
-                    nc.gpsimd.tensor_scalar(
-                        out=res[:, cols],
-                        in0=y[:, cols],
-                        scalar1=negmu[:],
-                        scalar2=rstd[:],
-                        op0=ALU.add,
-                        op1=ALU.mult,
-                    )
-                    nc.gpsimd.tensor_tensor(
-                        out=res[:, cols], in0=res[:, cols], in1=gamma_b[:, cols], op=ALU.mult
-                    )
-                    nc.gpsimd.tensor_tensor(
-                        out=res[:, cols], in0=res[:, cols], in1=beta_b[:, cols], op=ALU.add
-                    )
-                    nc.sync.dma_start(out=rows[:, cols], in_=res[:, cols])
-            else:
-                for cols in halves:
-                    nc.vector.scalar_tensor_tensor(
-                        out=res[:, cols],
-                        in0=y[:, cols],
-                        scalar=negmu[:],
-                        in1=gamma_b[:, cols],
-                        op0=ALU.add,
-                        op1=ALU.mult,
-                    )
-                for cols in halves:
-                    nc.vector.scalar_tensor_tensor(
-                        out=res[:, cols],
-                        in0=res[:, cols],
-                        scalar=rstd[:],
-                        in1=beta_b[:, cols],
-                        op0=ALU.mult,
-                        op1=ALU.add,
-                    )
-                    nc.sync.dma_start(out=rows[:, cols], in_=res[:, cols])
+        def half_statistics(n):
+            m = n // 2
+            if n % 2 == 0:
+                tiles["stats", m] = small.tile([P, 12], F32, tag="stats", name="stats")
+            nc.vector.bn_stats(
+                out=tiles["stats", m][:, (n % 2) * 6 : (n % 2 + 1) * 6],
+                in_=tiles["y", m][:, (n % 2) * 512 : (n % 2 + 1) * 512],
+            )
 
+        def aggregate(m):
+            mv = small.tile([P, 2], F32, tag="mv", name="mv")
+            nc.vector.bn_aggr(out=mv[:], in_=tiles["stats", m][:])
+            tiles["mean", m] = mv
+            inverse_deviation(m, mv[:, 1:2], 1.0)
+
+        halves = (slice(0, 512), slice(512, 1024))
+
+        def store(m, cols):
+            rows = out[m // TT, (m % TT) * P : (m % TT + 1) * P, :]
+            nc.sync.dma_start(out=rows[:, cols], in_=tiles["res", m][:, cols])
+
+        def normalise_gpsimd(m):
+            res = y_pool.tile([P, D], F32, tag="res", name="res")
+            tiles["res", m] = res
+            for cols in halves:
+                nc.gpsimd.tensor_scalar(
+                    out=res[:, cols],
+                    in0=tiles["y", m][:, cols],
+                    scalar1=tiles["negmu", m][:],
+                    scalar2=tiles["rstd", m][:],
+                    op0=ALU.add,
+                    op1=ALU.mult,
+                )
+            for cols in halves:
+                nc.gpsimd.tensor_tensor(
+                    out=res[:, cols], in0=res[:, cols], in1=gamma_b[:, cols], op=ALU.mult
+                )
+            for cols in halves:
+                nc.gpsimd.tensor_tensor(
+                    out=res[:, cols], in0=res[:, cols], in1=beta_b[:, cols], op=ALU.add
+                )
+                store(m, cols)
+
+        def center(m):
+            res = y_pool.tile([P, D], F32, tag="res", name="res")
+            tiles["res", m] = res
+            aggregated = ("mean", m) in tiles
+            for cols in halves:
+                nc.vector.scalar_tensor_tensor(
+                    out=res[:, cols],
+                    in0=tiles["y", m][:, cols],
+                    scalar=tiles["mean", m][:, 0:1] if aggregated else tiles["negmu", m][:],
+                    in1=gamma_b[:, cols],
+                    op0=ALU.subtract if aggregated else ALU.add,
+                    op1=ALU.mult,
+                )
+
+        def scale(m):
+            for cols in halves:
+                nc.vector.scalar_tensor_tensor(
+                    out=tiles["res", m][:, cols],
+                    in0=tiles["res", m][:, cols],
+                    scalar=tiles["rstd", m][:],
+                    in1=beta_b[:, cols],
+                    op0=ALU.mult,
+                    op1=ALU.add,
+                )
+                store(m, cols)
+
+        def ev_step(n):
+            return max(2 * n + 3, EV_FIRST + n) if n < HALVES // 2 else max(2 * n + 3, EV_SECOND + n - HALVES // 2)
+
+        plan = {}
+
+        def at(step, call, *args):
+            plan.setdefault(step, []).append((call, args))
+
+        last = UNITS - 1
+        for n in range(HALVES):
+            at(2 * n + 3, quantise_e, n)
+            at(ev_step(n), e_times_v, n)
+            at(ev_step(n) + 1, residual, n)
+        for m in range(UNITS):
+            s = ev_step(2 * m + 1) + 2
+            if m < UNITS - VECTOR_UNITS:
+                at(s, mean, m)
+                at(s, row_statistics, m)
+                at(s + 1, normalise_gpsimd, m)
+            elif m < last:
+                at(s, mean, m)
+                at(s + 1, row_statistics, m)
+                at(s + 2, center, m)
+                at(s + 4, scale, m)
+            else:
+                at(s - 2, half_statistics, 2 * m)
+                at(s - 1, half_statistics, 2 * m + 1)
+                at(s, aggregate, m)
+                at(s, center, m)
+                at(s + 1, scale, m)
         for j in range(AHEAD):
             scores(j)
             row_max(j)
         scores(AHEAD)
-        for step in range(PAIRS + 5):
+        for step in range(max(plan) + 1):
             if 0 <= step - 1 < PAIRS:
                 transpose_e(step - 1)
             if step + AHEAD + 1 < PAIRS:
@@ -524,14 +587,7 @@ def tile_multiheadattentionlayer_pa_kernel(
                 exponentials(step)
             if 0 <= step - 1 < PAIRS:
                 copy_e(step - 1)
-            if step >= 3 and step % 2 == 1 and (step - 3) // 2 < HALVES:
-                quantise_e((step - 3) // 2)
-                e_times_v((step - 3) // 2)
-            if step >= 4 and step % 2 == 0 and (step - 4) // 2 < HALVES:
-                residual((step - 4) // 2)
-            if step >= 7 and step % 4 == 3:
-                row_statistics((step - 7) // 4)
-            if step >= 8 and step % 4 == 0:
-                normalise((step - 8) // 4)
-            for i in range(JOBS_PER_STEP):
+            for call, args in plan.get(step, []):
+                call(*args)
+            for i in range(JOBS_FIRST if step < EV_FIRST else JOBS_PER_STEP):
                 advance()

@@ -26,14 +26,16 @@ UNITS = B * TT
 HALVES = UNITS * 2
 PAIRS = UNITS * 4
 JOBS_PER_STEP = 2
-EV_FIRST = 7
-EV_SECOND = 21
+EV_FIRST = 9
+EV_SECOND = 19
 JOBS_FIRST = 5
 AHEAD = 1
 SNEG_BUFS = 2 * AHEAD + 4
 VECTOR_UNITS = 2
-RELU_SPLIT = 4
-LEAD = 2
+VECTOR_EVERY = 4
+VECTOR_EVERY_LATE = 4
+SCALAR_MASKS = 0
+LEAD = 1
 
 FLOPS = 2 * B * S * D * D + 2 * 2 * B * H * S * S * DH
 
@@ -46,7 +48,7 @@ def tile_multiheadattentionlayer_pa_kernel(
         ctx.enter_context(tc.manual_schedule())
         const = ctx.enter_context(tc.tile_pool(name="const", bufs=1))
         keep = ctx.enter_context(tc.tile_pool(name="keep", bufs=1))
-        raw_pool = ctx.enter_context(tc.tile_pool(name="raw", bufs=8))
+        raw_pool = ctx.enter_context(tc.tile_pool(name="raw", bufs=9))
         grp_pool = ctx.enter_context(tc.tile_pool(name="grp", bufs=2))
         vt_pool = ctx.enter_context(tc.tile_pool(name="vt", bufs=3))
         s_pool = ctx.enter_context(tc.tile_pool(name="s", bufs=SNEG_BUFS))
@@ -56,8 +58,8 @@ def tile_multiheadattentionlayer_pa_kernel(
         y_pool = ctx.enter_context(tc.tile_pool(name="y", bufs=3))
         junk_pool = ctx.enter_context(tc.tile_pool(name="junk", bufs=2))
         small = ctx.enter_context(tc.tile_pool(name="small", bufs=8))
-        bank_psum = ctx.enter_context(tc.psum_pool(name="bank", bufs=5))
-        s_psum = ctx.enter_context(tc.psum_pool(name="sc", bufs=2))
+        bank_psum = ctx.enter_context(tc.psum_pool(name="bank", bufs=4))
+        s_psum = ctx.enter_context(tc.psum_pool(name="sc", bufs=3))
         o_psum = ctx.enter_context(tc.psum_pool(name="o", bufs=1))
 
         ident_b = const.tile([P, P], BF16)
@@ -93,23 +95,27 @@ def tile_multiheadattentionlayer_pa_kernel(
 
         raws = {}
 
-        def load(key, rows):
+        def load(name, b, src, first, count):
             raw = raw_pool.tile([P, 2 * D], BF16, tag="raw", name="raw")
+            raw_v = raw[:].rearrange("p (a k) -> p a k", a=2)
             nc.sync.dma_start(
-                out=raw[:].rearrange("p (a k) -> p a k", a=2),
-                in_=rows.rearrange("(a p) k -> p a k", p=P),
+                out=raw_v[:, 0:count, :],
+                in_=src[first * P : (first + count) * P, :].rearrange("(a p) k -> p a k", p=P),
             )
-            raws[key] = raw
+            for a in range(count):
+                raws[name, b, first + a] = raw[:, a * D : (a + 1) * D]
 
         def load_batch(name, src, b):
-            for a2 in range(2):
-                load((name, b, a2), src[b, a2 * 2 * P : (a2 + 1) * 2 * P, :])
+            for first in (0, 2):
+                load(name, b, src[b], first, 2)
 
+        load("q", 0, q_relu[0], 0, 1)
         load_batch("k", k_relu, 0)
-        load_batch("q", q_relu, 0)
         load_batch("keys", keys, 0)
-        for a2 in range(4):
-            load(("w", 0, a2), Wv[a2 * 2 * P : (a2 + 1) * 2 * P, :])
+        load("q", 0, q_relu[0], 1, 1)
+        for first in (0, 2, 4, 6):
+            load("w", 0, Wv, first, 2)
+        load("q", 0, q_relu[0], 2, 2)
         for b in range(B):
             nc.sync.dma_start(
                 out=x_v[:, b * TT : (b + 1) * TT, :],
@@ -123,6 +129,12 @@ def tile_multiheadattentionlayer_pa_kernel(
 
         tiles = {}
         done = set()
+
+        turn = {"copies": 0}
+
+        def vectors_turn(b):
+            turn["copies"] += 1
+            return turn["copies"] % (VECTOR_EVERY, VECTOR_EVERY_LATE)[b] == 0
 
         def word_transposes(key, words):
             bank = bank_psum.tile([P, 512], F32, tag="bank", name="bank")
@@ -142,33 +154,29 @@ def tile_multiheadattentionlayer_pa_kernel(
             return words.rearrange("p (a r u) -> p a r u", a=2, u=2)
 
         def heads_front(name, b, tt):
-            raw = raws[name, b, tt // 2]
             bank = bank_psum.tile([P, 1024], BF16, tag="bank", name="bank_b")
             for h in range(H):
-                first = (tt % 2) * D + h * DH
-                nc.tensor.transpose(
-                    bank[:, h * P : (h + 1) * P], raw[:, first : first + DH], ident_b[:]
-                )
+                cols = slice(h * DH, (h + 1) * DH)
+                nc.tensor.transpose(bank[:, cols], raws[name, b, tt][:, cols], ident_b[:])
             tiles[name, b, tt] = bank
 
         def heads_back(name, b, tt):
             dst = heads_T[name][:, b, :, tt * P : (tt + 1) * P]
             src = tiles[name, b, tt][:].rearrange("p (h r) -> p h r", h=H)
-            if name == "q":
+            if vectors_turn(b):
                 nc.vector.tensor_copy(out=dst, in_=src)
             else:
                 nc.scalar.copy(out=dst, in_=src)
             done.add((name, b, tt))
 
         def rows_front(name, b, t):
-            words = raws[name, b, t // 2][:].bitcast(F32)
-            word_transposes((name, b, t), words[:, (t % 2) * 512 : (t % 2 + 1) * 512])
+            word_transposes((name, b, t), raws[name, b, t].bitcast(F32))
 
         def keys_back(name, b, tt):
             if tt == 0:
                 tiles["kg", b] = grp_pool.tile([P, 4096], BF16, tag="grp", name="kg", align_bytes=64)
             kg_v = tiles["kg", b][:].bitcast(F32).rearrange("p (g s u) -> p g s u", g=2, u=2)
-            copy_interleaved((name, b, tt), kg_v[:, :, tt * P : (tt + 1) * P, :], tt == TT - 3)
+            copy_interleaved((name, b, tt), kg_v[:, :, tt * P : (tt + 1) * P, :], vectors_turn(b))
 
         def quantise_keys(b, c):
             cols = slice(b * 1024 + c * S, b * 1024 + (c + 1) * S)
@@ -187,7 +195,7 @@ def tile_multiheadattentionlayer_pa_kernel(
                 )
             wg_w = tiles["wg", ct // 4][:].bitcast(F32)
             copy_interleaved(
-                (name, b, ct), as_blocks(wg_w[:, (ct % 4) * 512 : (ct % 4 + 1) * 512]), ct % 4 == 1
+                (name, b, ct), as_blocks(wg_w[:, (ct % 4) * 512 : (ct % 4 + 1) * 512]), vectors_turn(b)
             )
 
         def quantise_w(half):
@@ -225,7 +233,7 @@ def tile_multiheadattentionlayer_pa_kernel(
             if h % 2 == 0:
                 tiles["vT", b, h // 2] = vt_pool.tile([P, 2 * S], BF16, tag="vt", name="vT")
             dst = tiles["vT", b, h // 2][:, (h % 2) * S : (h % 2 + 1) * S]
-            if h % RELU_SPLIT != RELU_SPLIT - 1:
+            if not vectors_turn(b):
                 nc.scalar.activation(
                     out=dst, in_=tiles["acc", b, h][:], func=ACT.Relu, bias=bvT[:, h : h + 1], scale=1.0
                 )
@@ -250,7 +258,7 @@ def tile_multiheadattentionlayer_pa_kernel(
                 )
             vg_w = tiles["vg", b, g // 2][:].bitcast(F32)
             copy_interleaved(
-                ("vbank", b, g), as_blocks(vg_w[:, (g % 2) * 512 : (g % 2 + 1) * 512]), g % 2 == 0
+                ("vbank", b, g), as_blocks(vg_w[:, (g % 2) * 512 : (g % 2 + 1) * 512]), vectors_turn(b)
             )
 
         def quantise_v(b, half):
@@ -264,42 +272,58 @@ def tile_multiheadattentionlayer_pa_kernel(
 
         def mask_rows(b, tt):
             mjunk = junk_pool.tile([P, D], BF16, tag="mjunk", name="mjunk")
-            nc.vector.tensor_scalar(
-                out=mjunk[:],
-                in0=x_v[:, b * TT + tt, :],
-                scalar1=0.0,
-                scalar2=None,
-                op0=ALU.not_equal,
-                op1=ALU.max,
-                accum_out=msk[:, tt * B + b : tt * B + b + 1],
-            )
+            anything = msk[:, tt * B + b : tt * B + b + 1]
+            if tt >= TT - SCALAR_MASKS:
+                nc.scalar.activation(
+                    out=mjunk[:], in_=x_v[:, b * TT + tt, :], func=ACT.Abs, accum_out=anything
+                )
+            else:
+                nc.vector.tensor_scalar(
+                    out=mjunk[:],
+                    in0=x_v[:, b * TT + tt, :],
+                    scalar1=0.0,
+                    scalar2=None,
+                    op0=ALU.not_equal,
+                    op1=ALU.max,
+                    accum_out=anything,
+                )
             done.add(("mask", b, tt))
 
+        def merged(copies, others):
+            out = []
+            for i, job in enumerate(copies):
+                out.append(job)
+                for k in range(len(others)):
+                    if (k + 1) * len(copies) // (len(others) + 1) == i:
+                        out.append(others[k])
+            return out
+
+        def only(call, *args):
+            return (None, call, args, ())
+
+        mask_jobs = [only(mask_rows, bb, tt) for tt in range(TT) for bb in range(B)]
         jobs = []
         for b in range(B):
-            for name in ("k", "q"):
-                jobs.extend([(heads_front, heads_back, (name, b, tt), ()) for tt in range(TT)])
+            jobs.append((heads_front, heads_back, ("q", b, 0), ()))
+            jobs.extend([(heads_front, heads_back, ("k", b, tt), ()) for tt in range(TT)])
+            later_q = [(heads_front, heads_back, ("q", b, tt), ()) for tt in range(1, TT)]
             jobs.extend([(rows_front, keys_back, ("keys", b, tt), ()) for tt in range(TT)])
-            jobs.extend([(None, quantise_keys, (b, c), ()) for c in range(2)])
+            quantised = [only(quantise_keys, b, c) for c in range(2)]
+            projected = [
+                (project_front, project_back, (b, h), (("keys", b), ("w", h // 4))) for h in range(H)
+            ]
+            turned = [(v_front, v_back, (b, g), (("vT", b, 2 * g + 1),)) for g in range(4)]
             if b == 0:
+                weights = [(rows_front, w_back, ("w", 0, ct), ()) for ct in range(H)]
                 jobs.append((bias_front, bias_back, (), ()))
-                for half in range(2):
-                    jobs.extend(
-                        [(rows_front, w_back, ("w", 0, half * 4 + c4), ()) for c4 in range(4)]
-                    )
-                    jobs.append((None, quantise_w, (half,), ()))
-                jobs.extend([(None, mask_rows, (bb, 0), ()) for bb in range(B)])
-            jobs.extend(
-                [
-                    (project_front, project_back, (b, h), (("keys", b), ("w", h // 4)))
-                    for h in range(H)
-                ]
-            )
-            jobs.extend([(v_front, v_back, (b, g), (("vT", b, 2 * g + 1),)) for g in range(4)])
-            jobs.extend([(None, quantise_v, (b, half), ()) for half in range(2)])
-            if b == 0:
-                for tt in range(1, TT):
-                    jobs.extend([(None, mask_rows, (bb, tt), ()) for bb in range(B)])
+                jobs.extend(merged(later_q[:1] + weights[:4], quantised + mask_jobs[:2]))
+                jobs.extend(merged(weights[4:], [only(quantise_w, 0)] + mask_jobs[2:5]))
+                jobs.extend(merged(later_q[1:], mask_jobs[5:6]) + [only(quantise_w, 1)])
+                jobs.extend(merged(projected[:6], mask_jobs[6:8]))
+            else:
+                jobs.extend(merged(later_q, quantised))
+                jobs.extend(projected[:6])
+            jobs.extend(turned[:2] + projected[6:] + [only(quantise_v, b, 0)] + turned[2:] + [only(quantise_v, b, 1)])
         issued = {"front": 0, "back": 0}
 
         def advance():
@@ -335,8 +359,11 @@ def tile_multiheadattentionlayer_pa_kernel(
                 )
                 tiles["s", k] = s_bank
 
-        def row_max(j):
+        def row_max(j, between=()):
             for k in (2 * j, 2 * j + 1):
+                if k % 2 == 1:
+                    for call, args in between:
+                        call(*args)
                 sneg = s_pool.tile([P, S], F32, tag="sneg", name="sneg")
                 nbias = small.tile([P, 1], F32, tag="nbias", name="nbias", bufs=SNEG_BUFS)
                 nc.vector.tensor_scalar(
@@ -352,8 +379,8 @@ def tile_multiheadattentionlayer_pa_kernel(
                 tiles["nbias", k] = nbias
 
         def exponentials(j):
-            if j % 2 == 0:
-                tiles["rowsum", j // 2] = small.tile([P, 4], F32, tag="rowsum", name="rowsum")
+            if j % 4 == 0:
+                tiles["rowsum", j // 4] = small.tile([P, H], F32, tag="rowsum", name="rowsum")
             e2 = e_pool.tile([P, 2 * S], BF16, tag="e", name="e2")
             for hh in range(2):
                 k = 2 * j + hh
@@ -363,7 +390,7 @@ def tile_multiheadattentionlayer_pa_kernel(
                     func=ACT.Exp,
                     bias=tiles["nbias", k][:],
                     scale=-1.0,
-                    accum_out=tiles["rowsum", j // 2][:, k % 4 : k % 4 + 1],
+                    accum_out=tiles["rowsum", j // 4][:, k % H : k % H + 1],
                 )
             tiles["e", j] = e2
 
@@ -381,24 +408,11 @@ def tile_multiheadattentionlayer_pa_kernel(
             )
 
         def quantise_e(n):
-            it = (n // 2) % TT
-            need(("mask", 0, it))
-            need(("mask", 1, it))
-            rinv = small.tile([P, 4], F32, tag="rinv", name="rinv")
-            nc.vector.reciprocal(out=rinv[:], in_=tiles["rowsum", n][:])
-            r = small.tile([P, 4], F32, tag="r", name="r")
             e_codes = ec_pool.tile([P, 512], U32, tag="ec", name="e_codes", align_bytes=64)
             e_scales = ec_pool.tile([P, 512], U8, tag="es", name="e_scales", align_bytes=64)
             nc.vector.quantize_mx(
                 out=e_codes[:].bitcast(FP8X4), scales=e_scales[:], in_=tiles["eg", n][:]
             )
-            nc.vector.tensor_tensor(
-                out=r[:].rearrange("p (a c) -> p a c", a=2),
-                in0=rinv[:].rearrange("p (a c) -> p a c", a=2),
-                in1=msk[:, it * B : (it + 1) * B].unsqueeze(1).to_broadcast([P, 2, B]),
-                op=ALU.mult,
-            )
-            tiles["r", n] = r
             tiles["ec", n] = e_codes
             tiles["es", n] = e_scales
 
@@ -421,6 +435,26 @@ def tile_multiheadattentionlayer_pa_kernel(
                 )
             tiles["o", n] = o_bank
 
+        def reciprocals(m):
+            rinv = small.tile([P, H], F32, tag="rinv", name="rinv")
+            nc.vector.reciprocal(out=rinv[:], in_=tiles["rowsum", m][:])
+            tiles["rinv", m] = rinv
+
+        def masked_reciprocals(m):
+            it = m % TT
+            need(("mask", 0, it))
+            need(("mask", 1, it))
+            r = small.tile([P, H], F32, tag="r", name="r")
+            nc.vector.scalar_tensor_tensor(
+                out=r[:].rearrange("p (a c) -> p a c", c=B),
+                in0=msk[:, it * B : (it + 1) * B].unsqueeze(1).to_broadcast([P, H // B, B]),
+                scalar=0.0,
+                in1=tiles["rinv", m][:].rearrange("p (a c) -> p a c", c=B),
+                op0=ALU.not_equal,
+                op1=ALU.mult,
+            )
+            tiles["r", m] = r
+
         def residual(n):
             m = n // 2
             if n % 2 == 0:
@@ -431,12 +465,13 @@ def tile_multiheadattentionlayer_pa_kernel(
                 nc.vector.scalar_tensor_tensor(
                     out=tiles["y", m][:, h * DH : (h + 1) * DH],
                     in0=tiles["o", n][:, h4 * P : (h4 + 1) * P],
-                    scalar=tiles["r", n][:, h4 : h4 + 1],
+                    scalar=tiles["r", m][:, h : h + 1],
                     in1=x_v[:, m, h * DH : (h + 1) * DH],
                     op0=ALU.mult,
                     op1=ALU.add,
-                    accum_out=tiles["ysum", m][:, h : h + 1],
+                    accum_out=tiles["ysum", m][:, h : h + 1] if m < UNITS - 1 else None,
                 )
+
         def mean(m):
             junk8 = small.tile([P, H], F32, tag="junk8", name="junk8")
             negmu = small.tile([P, 1], F32, tag="negmu", name="negmu")
@@ -494,10 +529,11 @@ def tile_multiheadattentionlayer_pa_kernel(
             rows = out[m // TT, (m % TT) * P : (m % TT + 1) * P, :]
             nc.sync.dma_start(out=rows[:, cols], in_=tiles["res", m][:, cols])
 
-        def normalise_gpsimd(m):
-            res = y_pool.tile([P, D], F32, tag="res", name="res")
-            tiles["res", m] = res
-            for cols in halves:
+        def normalise_gpsimd(m, parts):
+            if ("res", m) not in tiles:
+                tiles["res", m] = y_pool.tile([P, D], F32, tag="res", name="res")
+            res = tiles["res", m]
+            for cols in parts:
                 nc.gpsimd.tensor_scalar(
                     out=res[:, cols],
                     in0=tiles["y", m][:, cols],
@@ -506,21 +542,22 @@ def tile_multiheadattentionlayer_pa_kernel(
                     op0=ALU.add,
                     op1=ALU.mult,
                 )
-            for cols in halves:
+            for cols in parts:
                 nc.gpsimd.tensor_tensor(
                     out=res[:, cols], in0=res[:, cols], in1=gamma_b[:, cols], op=ALU.mult
                 )
-            for cols in halves:
+            for cols in parts:
                 nc.gpsimd.tensor_tensor(
                     out=res[:, cols], in0=res[:, cols], in1=beta_b[:, cols], op=ALU.add
                 )
                 store(m, cols)
 
-        def center(m):
-            res = y_pool.tile([P, D], F32, tag="res", name="res")
-            tiles["res", m] = res
+        def center(m, parts):
+            if ("res", m) not in tiles:
+                tiles["res", m] = y_pool.tile([P, D], F32, tag="res", name="res")
+            res = tiles["res", m]
             aggregated = ("mean", m) in tiles
-            for cols in halves:
+            for cols in parts:
                 nc.vector.scalar_tensor_tensor(
                     out=res[:, cols],
                     in0=tiles["y", m][:, cols],
@@ -530,8 +567,8 @@ def tile_multiheadattentionlayer_pa_kernel(
                     op1=ALU.mult,
                 )
 
-        def scale(m):
-            for cols in halves:
+        def scale(m, parts):
+            for cols in parts:
                 nc.vector.scalar_tensor_tensor(
                     out=tiles["res", m][:, cols],
                     in0=tiles["res", m][:, cols],
@@ -546,11 +583,15 @@ def tile_multiheadattentionlayer_pa_kernel(
             return max(2 * n + 3, EV_FIRST + n) if n < HALVES // 2 else max(2 * n + 3, EV_SECOND + n - HALVES // 2)
 
         plan = {}
+        among = {}
 
         def at(step, call, *args):
             plan.setdefault(step, []).append((call, args))
 
         last = UNITS - 1
+        for m in range(UNITS):
+            among[4 * m + 4] = [(reciprocals, (m,))]
+            at(ev_step(2 * m) + 1, masked_reciprocals, m)
         for n in range(HALVES):
             at(2 * n + 3, quantise_e, n)
             at(ev_step(n), e_times_v, n)
@@ -560,18 +601,19 @@ def tile_multiheadattentionlayer_pa_kernel(
             if m < UNITS - VECTOR_UNITS:
                 at(s, mean, m)
                 at(s, row_statistics, m)
-                at(s + 1, normalise_gpsimd, m)
+                at(s + 1, normalise_gpsimd, m, halves)
             elif m < last:
                 at(s, mean, m)
                 at(s + 1, row_statistics, m)
-                at(s + 2, center, m)
-                at(s + 4, scale, m)
+                at(s + 2, center, m, halves[:1])
+                at(s + 2, normalise_gpsimd, m, halves[1:])
+                at(s + 4, scale, m, halves[:1])
             else:
                 at(s - 2, half_statistics, 2 * m)
                 at(s - 1, half_statistics, 2 * m + 1)
                 at(s, aggregate, m)
-                at(s, center, m)
-                at(s + 1, scale, m)
+                at(s, center, m, halves)
+                at(s + 1, scale, m, halves)
         for j in range(AHEAD):
             scores(j)
             row_max(j)
@@ -582,7 +624,10 @@ def tile_multiheadattentionlayer_pa_kernel(
             if step + AHEAD + 1 < PAIRS:
                 scores(step + AHEAD + 1)
             if step + AHEAD < PAIRS:
-                row_max(step + AHEAD)
+                row_max(step + AHEAD, among.get(step, []))
+            else:
+                for call, args in among.get(step, []):
+                    call(*args)
             if step < PAIRS:
                 exponentials(step)
             if 0 <= step - 1 < PAIRS:

@@ -26,14 +26,15 @@ UNITS = B * TT
 HALVES = UNITS * 2
 PAIRS = UNITS * 4
 JOBS_PER_STEP = 2
-EV_FIRST = 9
+EV_FIRST = 7
 EV_SECOND = 19
-JOBS_FIRST = 5
+JOBS_FIRST = 6
 AHEAD = 1
 SNEG_BUFS = 2 * AHEAD + 4
 VECTOR_UNITS = 2
-VECTOR_EVERY = 4
-VECTOR_EVERY_LATE = 4
+VECTOR_EVERY = 100
+SCALAR_HEADS = (("pair", 0), ("k", 1, 1), ("k", 1, 3))
+VECTOR_EVERY_LATE = 3
 SCALAR_MASKS = 0
 LEAD = 1
 
@@ -48,7 +49,7 @@ def tile_multiheadattentionlayer_pa_kernel(
         ctx.enter_context(tc.manual_schedule())
         const = ctx.enter_context(tc.tile_pool(name="const", bufs=1))
         keep = ctx.enter_context(tc.tile_pool(name="keep", bufs=1))
-        raw_pool = ctx.enter_context(tc.tile_pool(name="raw", bufs=9))
+        raw_pool = ctx.enter_context(tc.tile_pool(name="raw", bufs=8))
         grp_pool = ctx.enter_context(tc.tile_pool(name="grp", bufs=2))
         vt_pool = ctx.enter_context(tc.tile_pool(name="vt", bufs=3))
         s_pool = ctx.enter_context(tc.tile_pool(name="s", bufs=SNEG_BUFS))
@@ -109,8 +110,18 @@ def tile_multiheadattentionlayer_pa_kernel(
             for first in (0, 2):
                 load(name, b, src[b], first, 2)
 
+        def load_pair(g):
+            raw = raw_pool.tile([P, TT * 2 * DH], BF16, tag="rawk", name="rawk", bufs=4)
+            nc.sync.dma_start(
+                out=raw[:].rearrange("p (t k) -> p t k", t=TT),
+                in_=k_relu[0][:, g * 2 * DH : (g + 1) * 2 * DH].rearrange("(t p) k -> p t k", p=P),
+            )
+            raws["k", 0, "pair", g] = raw
+
+        load_pair(0)
         load("q", 0, q_relu[0], 0, 1)
-        load_batch("k", k_relu, 0)
+        for g in range(1, H // 2):
+            load_pair(g)
         load_batch("keys", keys, 0)
         load("q", 0, q_relu[0], 1, 1)
         for first in (0, 2, 4, 6):
@@ -160,10 +171,32 @@ def tile_multiheadattentionlayer_pa_kernel(
                 nc.tensor.transpose(bank[:, cols], raws[name, b, tt][:, cols], ident_b[:])
             tiles[name, b, tt] = bank
 
+        def pair_front(g):
+            bank = bank_psum.tile([P, 1024], BF16, tag="bank", name="bank_p")
+            for hh in range(2):
+                for tt in range(TT):
+                    first = tt * 2 * DH + hh * DH
+                    block = (hh * TT + tt) * P
+                    nc.tensor.transpose(
+                        bank[:, block : block + P],
+                        raws["k", 0, "pair", g][:, first : first + DH],
+                        ident_b[:],
+                    )
+            tiles["pair", g] = bank
+
+        def pair_back(g):
+            dst = heads_T["k"][:, 0, 2 * g : 2 * g + 2, :]
+            src = tiles["pair", g][:].rearrange("p (h r) -> p h r", h=2)
+            if ("pair", g) not in SCALAR_HEADS:
+                nc.vector.tensor_copy(out=dst, in_=src)
+            else:
+                nc.scalar.copy(out=dst, in_=src)
+            done.add(("k", 0, "pair", g))
+
         def heads_back(name, b, tt):
             dst = heads_T[name][:, b, :, tt * P : (tt + 1) * P]
             src = tiles[name, b, tt][:].rearrange("p (h r) -> p h r", h=H)
-            if vectors_turn(b):
+            if (name, b, tt) not in SCALAR_HEADS:
                 nc.vector.tensor_copy(out=dst, in_=src)
             else:
                 nc.scalar.copy(out=dst, in_=src)
@@ -304,8 +337,13 @@ def tile_multiheadattentionlayer_pa_kernel(
         mask_jobs = [only(mask_rows, bb, tt) for tt in range(TT) for bb in range(B)]
         jobs = []
         for b in range(B):
-            jobs.append((heads_front, heads_back, ("q", b, 0), ()))
-            jobs.extend([(heads_front, heads_back, ("k", b, tt), ()) for tt in range(TT)])
+            if b == 0:
+                jobs.append((pair_front, pair_back, (0,), ()))
+                jobs.append((heads_front, heads_back, ("q", b, 0), ()))
+                jobs.extend([(pair_front, pair_back, (g,), ()) for g in range(1, H // 2)])
+            else:
+                jobs.append((heads_front, heads_back, ("q", b, 0), ()))
+                jobs.extend([(heads_front, heads_back, ("k", b, tt), ()) for tt in range(TT)])
             later_q = [(heads_front, heads_back, ("q", b, tt), ()) for tt in range(1, TT)]
             jobs.extend([(rows_front, keys_back, ("keys", b, tt), ()) for tt in range(TT)])
             quantised = [only(quantise_keys, b, c) for c in range(2)]
@@ -347,7 +385,7 @@ def tile_multiheadattentionlayer_pa_kernel(
         def scores(j):
             for k in (2 * j, 2 * j + 1):
                 b, it, h = k // (H * TT), (k // H) % TT, k % H
-                need(("k", b, TT - 1))
+                need(("k", b, "pair", h // 2) if b == 0 else ("k", b, TT - 1))
                 need(("q", b, it))
                 s_bank = s_psum.tile([P, S], F32, tag="s", name="s_bank")
                 nc.tensor.matmul(
@@ -521,13 +559,24 @@ def tile_multiheadattentionlayer_pa_kernel(
             mv = small.tile([P, 2], F32, tag="mv", name="mv")
             nc.vector.bn_aggr(out=mv[:], in_=tiles["stats", m][:])
             tiles["mean", m] = mv
-            inverse_deviation(m, mv[:, 1:2], 1.0)
+            deviation = small.tile([P, 1], F32, tag="deviation", name="deviation")
+            nc.scalar.activation(out=deviation[:], in_=mv[:, 1:2], func=ACT.Sqrt, bias=LN_EPS, scale=1.0)
+            tiles["deviation", m] = deviation
+
+        def invert(m):
+            rstd = small.tile([P, 1], F32, tag="rstd", name="rstd")
+            nc.vector.reciprocal(out=rstd[:], in_=tiles["deviation", m][:])
+            tiles["rstd", m] = rstd
+
+        def warm_sqrt():
+            nc.scalar.activation(out=warm[:], in_=warm[:], func=ACT.Sqrt)
 
         halves = (slice(0, 512), slice(512, 1024))
+        QUARTERS = tuple(slice(c, c + 256) for c in range(0, D, 256))
 
-        def store(m, cols):
+        def store(m, cols, queue=nc.sync):
             rows = out[m // TT, (m % TT) * P : (m % TT + 1) * P, :]
-            nc.sync.dma_start(out=rows[:, cols], in_=tiles["res", m][:, cols])
+            queue.dma_start(out=rows[:, cols], in_=tiles["res", m][:, cols])
 
         def normalise_gpsimd(m, parts):
             if ("res", m) not in tiles:
@@ -550,7 +599,8 @@ def tile_multiheadattentionlayer_pa_kernel(
                 nc.gpsimd.tensor_tensor(
                     out=res[:, cols], in0=res[:, cols], in1=beta_b[:, cols], op=ALU.add
                 )
-                store(m, cols)
+                if m < UNITS - VECTOR_UNITS:
+                    store(m, cols)
 
         def center(m, parts):
             if ("res", m) not in tiles:
@@ -611,9 +661,12 @@ def tile_multiheadattentionlayer_pa_kernel(
             else:
                 at(s - 2, half_statistics, 2 * m)
                 at(s - 1, half_statistics, 2 * m + 1)
-                at(s, aggregate, m)
+                at(s - 1, warm_sqrt)
+                at(s - 1, aggregate, m)
                 at(s, center, m, halves)
-                at(s + 1, scale, m, halves)
+                at(s, invert, m)
+                at(s, store, m - 1, halves[1], nc.scalar)
+                at(s + 1, scale, m, QUARTERS)
         for j in range(AHEAD):
             scores(j)
             row_max(j)

@@ -32,10 +32,11 @@ JOBS_FIRST = 6
 AHEAD = 1
 SNEG_BUFS = 2 * AHEAD + 4
 VECTOR_UNITS = 2
-VECTOR_EVERY = 100
-SCALAR_HEADS = (("pair", 0), ("k", 1, 1), ("k", 1, 3))
-VECTOR_EVERY_LATE = 3
+EVERY = {("keys", 0): 2, ("keys", 1): 3, ("w", 0): 100, ("relu", 0): 4, ("relu", 1): 3, ("v", 0): 100, ("v", 1): 3}
+SCALAR_HEADS = (("pair", 2), ("q", 0, 2), ("k", 1, 1), ("k", 1, 3), ("q", 1, 1), ("q", 1, 3))
 SCALAR_MASKS = 0
+MASKS_AT = (1, 4, 6)
+BIAS_LATER = 0
 LEAD = 1
 
 FLOPS = 2 * B * S * D * D + 2 * 2 * B * H * S * S * DH
@@ -118,8 +119,11 @@ def tile_multiheadattentionlayer_pa_kernel(
             )
             raws["k", 0, "pair", g] = raw
 
+        first_q = raw_pool.tile([P, D], BF16, tag="rawq", name="rawq", bufs=1)
+        first_cols = (slice(0, 2 * DH), slice(2 * DH, D))
+        nc.sync.dma_start(out=first_q[:, first_cols[0]], in_=q_relu[0][0:P, first_cols[0]])
         load_pair(0)
-        load("q", 0, q_relu[0], 0, 1)
+        nc.sync.dma_start(out=first_q[:, first_cols[1]], in_=q_relu[0][0:P, first_cols[1]])
         for g in range(1, H // 2):
             load_pair(g)
         load_batch("keys", keys, 0)
@@ -141,11 +145,12 @@ def tile_multiheadattentionlayer_pa_kernel(
         tiles = {}
         done = set()
 
-        turn = {"copies": 0}
+        turn = {}
 
-        def vectors_turn(b):
-            turn["copies"] += 1
-            return turn["copies"] % (VECTOR_EVERY, VECTOR_EVERY_LATE)[b] == 0
+        def vectors_turn(b, kind):
+            key = (kind, b)
+            turn[key] = turn.get(key, 0) + 1
+            return turn[key] % EVERY[key] == 0
 
         def word_transposes(key, words):
             bank = bank_psum.tile([P, 512], F32, tag="bank", name="bank")
@@ -187,11 +192,30 @@ def tile_multiheadattentionlayer_pa_kernel(
         def pair_back(g):
             dst = heads_T["k"][:, 0, 2 * g : 2 * g + 2, :]
             src = tiles["pair", g][:].rearrange("p (h r) -> p h r", h=2)
-            if ("pair", g) not in SCALAR_HEADS:
+            if g == 0:
+                nc.vector.tensor_copy(out=dst[:, 0, :], in_=src[:, 0, :])
+                nc.scalar.copy(out=dst[:, 1, :], in_=src[:, 1, :])
+            elif ("pair", g) not in SCALAR_HEADS:
                 nc.vector.tensor_copy(out=dst, in_=src)
             else:
                 nc.scalar.copy(out=dst, in_=src)
             done.add(("k", 0, "pair", g))
+
+        def first_front(part):
+            cols = first_cols[part]
+            bank = bank_psum.tile([P, 1024], BF16, tag="bank", name="bank_q")
+            for first in range(cols.start, cols.stop, DH):
+                nc.tensor.transpose(bank[:, first : first + DH], first_q[:, first : first + DH], ident_b[:])
+            tiles["first", part] = bank
+
+        def first_back(part):
+            cols = first_cols[part]
+            heads = slice(cols.start // DH, cols.stop // DH)
+            nc.vector.tensor_copy(
+                out=heads_T["q"][:, 0, heads, 0:P],
+                in_=tiles["first", part][:, cols].rearrange("p (h r) -> p h r", r=P),
+            )
+            done.add(("q", 0, 0, part))
 
         def heads_back(name, b, tt):
             dst = heads_T[name][:, b, :, tt * P : (tt + 1) * P]
@@ -209,7 +233,7 @@ def tile_multiheadattentionlayer_pa_kernel(
             if tt == 0:
                 tiles["kg", b] = grp_pool.tile([P, 4096], BF16, tag="grp", name="kg", align_bytes=64)
             kg_v = tiles["kg", b][:].bitcast(F32).rearrange("p (g s u) -> p g s u", g=2, u=2)
-            copy_interleaved((name, b, tt), kg_v[:, :, tt * P : (tt + 1) * P, :], vectors_turn(b))
+            copy_interleaved((name, b, tt), kg_v[:, :, tt * P : (tt + 1) * P, :], vectors_turn(b, "keys"))
 
         def quantise_keys(b, c):
             cols = slice(b * 1024 + c * S, b * 1024 + (c + 1) * S)
@@ -228,7 +252,7 @@ def tile_multiheadattentionlayer_pa_kernel(
                 )
             wg_w = tiles["wg", ct // 4][:].bitcast(F32)
             copy_interleaved(
-                (name, b, ct), as_blocks(wg_w[:, (ct % 4) * 512 : (ct % 4 + 1) * 512]), vectors_turn(b)
+                (name, b, ct), as_blocks(wg_w[:, (ct % 4) * 512 : (ct % 4 + 1) * 512]), vectors_turn(b, "w")
             )
 
         def quantise_w(half):
@@ -266,7 +290,7 @@ def tile_multiheadattentionlayer_pa_kernel(
             if h % 2 == 0:
                 tiles["vT", b, h // 2] = vt_pool.tile([P, 2 * S], BF16, tag="vt", name="vT")
             dst = tiles["vT", b, h // 2][:, (h % 2) * S : (h % 2 + 1) * S]
-            if not vectors_turn(b):
+            if not vectors_turn(b, "relu"):
                 nc.scalar.activation(
                     out=dst, in_=tiles["acc", b, h][:], func=ACT.Relu, bias=bvT[:, h : h + 1], scale=1.0
                 )
@@ -291,7 +315,7 @@ def tile_multiheadattentionlayer_pa_kernel(
                 )
             vg_w = tiles["vg", b, g // 2][:].bitcast(F32)
             copy_interleaved(
-                ("vbank", b, g), as_blocks(vg_w[:, (g % 2) * 512 : (g % 2 + 1) * 512]), vectors_turn(b)
+                ("vbank", b, g), as_blocks(vg_w[:, (g % 2) * 512 : (g % 2 + 1) * 512]), vectors_turn(b, "v")
             )
 
         def quantise_v(b, half):
@@ -338,8 +362,9 @@ def tile_multiheadattentionlayer_pa_kernel(
         jobs = []
         for b in range(B):
             if b == 0:
+                jobs.append((first_front, first_back, (0,), ()))
                 jobs.append((pair_front, pair_back, (0,), ()))
-                jobs.append((heads_front, heads_back, ("q", b, 0), ()))
+                jobs.append((first_front, first_back, (1,), ()))
                 jobs.extend([(pair_front, pair_back, (g,), ()) for g in range(1, H // 2)])
             else:
                 jobs.append((heads_front, heads_back, ("q", b, 0), ()))
@@ -353,11 +378,13 @@ def tile_multiheadattentionlayer_pa_kernel(
             turned = [(v_front, v_back, (b, g), (("vT", b, 2 * g + 1),)) for g in range(4)]
             if b == 0:
                 weights = [(rows_front, w_back, ("w", 0, ct), ()) for ct in range(H)]
-                jobs.append((bias_front, bias_back, (), ()))
-                jobs.extend(merged(later_q[:1] + weights[:4], quantised + mask_jobs[:2]))
-                jobs.extend(merged(weights[4:], [only(quantise_w, 0)] + mask_jobs[2:5]))
-                jobs.extend(merged(later_q[1:], mask_jobs[5:6]) + [only(quantise_w, 1)])
-                jobs.extend(merged(projected[:6], mask_jobs[6:8]))
+                bias_at = len(jobs) + BIAS_LATER
+                m1, m2, m3 = MASKS_AT
+                jobs.extend(merged(later_q[:1] + weights[:4], quantised + mask_jobs[:m1]))
+                jobs.extend(merged(weights[4:], [only(quantise_w, 0)] + mask_jobs[m1:m2]))
+                jobs.extend(merged(later_q[1:], mask_jobs[m2:m3]) + [only(quantise_w, 1)])
+                jobs.insert(bias_at, (bias_front, bias_back, (), ()))
+                jobs.extend(merged(projected[:6], mask_jobs[m3:8]))
             else:
                 jobs.extend(merged(later_q, quantised))
                 jobs.extend(projected[:6])
@@ -386,7 +413,7 @@ def tile_multiheadattentionlayer_pa_kernel(
             for k in (2 * j, 2 * j + 1):
                 b, it, h = k // (H * TT), (k // H) % TT, k % H
                 need(("k", b, "pair", h // 2) if b == 0 else ("k", b, TT - 1))
-                need(("q", b, it))
+                need(("q", b, it) if (b, it) != (0, 0) else ("q", 0, 0, min(h // 2, 1)))
                 s_bank = s_psum.tile([P, S], F32, tag="s", name="s_bank")
                 nc.tensor.matmul(
                     out=s_bank[:],

@@ -32,10 +32,11 @@ JOBS_FIRST = 6
 AHEAD = 1
 SNEG_BUFS = 2 * AHEAD + 4
 VECTOR_UNITS = 2
-EVERY = {("keys", 0): 2, ("keys", 1): 3, ("w", 0): 100, ("relu", 0): 4, ("relu", 1): 3, ("v", 0): 100, ("v", 1): 3}
-SCALAR_HEADS = (("pair", 2), ("q", 0, 2), ("k", 1, 1), ("k", 1, 3), ("q", 1, 1), ("q", 1, 3))
+EVERY = {("keys", 0): 2, ("keys", 1): 3, ("w", 0): 100, ("relu", 0): 100, ("relu", 1): 3, ("v", 0): 100, ("v", 1): 3}
+SCALAR_HEADS = (("pair", 1), ("pair", 3), ("q", 0, 1), ("q", 0, 3), ("k", 1, 0), ("k", 1, 1), ("k", 1, 3), ("q", 1, 1), ("q", 1, 3))
 SCALAR_MASKS = 0
-MASKS_AT = (1, 4, 6)
+X_TILES = 2
+MASKS_AT = (0, 0, 0)
 BIAS_LATER = 0
 LEAD = 1
 
@@ -131,11 +132,12 @@ def tile_multiheadattentionlayer_pa_kernel(
         for first in (0, 2, 4, 6):
             load("w", 0, Wv, first, 2)
         load("q", 0, q_relu[0], 2, 2)
-        for b in range(B):
-            nc.sync.dma_start(
-                out=x_v[:, b * TT : (b + 1) * TT, :],
-                in_=queries[b].rearrange("(t p) k -> p t k", p=P),
-            )
+        for tt in range(0, TT, X_TILES):
+            for b in range(B):
+                nc.sync.dma_start(
+                    out=x_v[:, b * TT + tt : b * TT + tt + X_TILES, :],
+                    in_=queries[b][tt * P : (tt + X_TILES) * P, :].rearrange("(t p) k -> p t k", p=P),
+                )
         load_batch("keys", keys, 1)
         nc.sync.dma_start(out=gamma_b[:], in_=ln_gamma.partition_broadcast(P))
         nc.sync.dma_start(out=beta_b[:], in_=ln_beta.partition_broadcast(P))

@@ -29,12 +29,17 @@ JOBS_PER_STEP = 2
 EV_FIRST = 7
 EV_SECOND = 19
 JOBS_FIRST = 6
+STAT_PARTS = ((0, 4), (4, 6), (6, 8))
 AHEAD = 1
 SNEG_BUFS = 2 * AHEAD + 4
 VECTOR_UNITS = 2
-EVERY = {("keys", 0): 2, ("keys", 1): 3, ("w", 0): 100, ("relu", 0): 100, ("relu", 1): 3, ("v", 0): 100, ("v", 1): 3}
+EVERY = {("keys", 0): 2, ("keys", 1): 3, ("w", 0): 4, ("relu", 0): 100, ("relu", 1): 3, ("v", 0): 100, ("v", 1): 3}
 SCALAR_HEADS = (("pair", 1), ("pair", 3), ("q", 0, 1), ("q", 0, 3), ("k", 1, 0), ("k", 1, 1), ("k", 1, 3), ("q", 1, 1), ("q", 1, 3))
 SCALAR_MASKS = 0
+CENTER = 1
+RECIP = 2
+MASKED = 2
+R_EARLY = 0
 X_TILES = 2
 MASKS_AT = (0, 0, 0)
 BIAS_LATER = 0
@@ -60,7 +65,7 @@ def tile_multiheadattentionlayer_pa_kernel(
         ec_pool = ctx.enter_context(tc.tile_pool(name="ec", bufs=6))
         y_pool = ctx.enter_context(tc.tile_pool(name="y", bufs=3))
         junk_pool = ctx.enter_context(tc.tile_pool(name="junk", bufs=2))
-        small = ctx.enter_context(tc.tile_pool(name="small", bufs=8))
+        small = ctx.enter_context(tc.tile_pool(name="small", bufs=12))
         bank_psum = ctx.enter_context(tc.psum_pool(name="bank", bufs=4))
         s_psum = ctx.enter_context(tc.psum_pool(name="sc", bufs=3))
         o_psum = ctx.enter_context(tc.psum_pool(name="o", bufs=1))
@@ -98,45 +103,48 @@ def tile_multiheadattentionlayer_pa_kernel(
 
         raws = {}
 
-        def load(name, b, src, first, count):
+        def tokens(rows):
+            return rows.rearrange("(p t) k -> p t k", t=TT)
+
+        def load(name, b, tiled, first, count):
             raw = raw_pool.tile([P, 2 * D], BF16, tag="raw", name="raw")
             raw_v = raw[:].rearrange("p (a k) -> p a k", a=2)
             nc.sync.dma_start(
                 out=raw_v[:, 0:count, :],
-                in_=src[first * P : (first + count) * P, :].rearrange("(a p) k -> p a k", p=P),
+                in_=tiled[:, first : first + count, :],
             )
             for a in range(count):
                 raws[name, b, first + a] = raw[:, a * D : (a + 1) * D]
 
         def load_batch(name, src, b):
             for first in (0, 2):
-                load(name, b, src[b], first, 2)
+                load(name, b, tokens(src[b]), first, 2)
 
         def load_pair(g):
             raw = raw_pool.tile([P, TT * 2 * DH], BF16, tag="rawk", name="rawk", bufs=4)
             nc.sync.dma_start(
                 out=raw[:].rearrange("p (t k) -> p t k", t=TT),
-                in_=k_relu[0][:, g * 2 * DH : (g + 1) * 2 * DH].rearrange("(t p) k -> p t k", p=P),
+                in_=tokens(k_relu[0])[:, :, g * 2 * DH : (g + 1) * 2 * DH],
             )
             raws["k", 0, "pair", g] = raw
 
         first_q = raw_pool.tile([P, D], BF16, tag="rawq", name="rawq", bufs=1)
         first_cols = (slice(0, 2 * DH), slice(2 * DH, D))
-        nc.sync.dma_start(out=first_q[:, first_cols[0]], in_=q_relu[0][0:P, first_cols[0]])
+        nc.sync.dma_start(out=first_q[:, first_cols[0]], in_=tokens(q_relu[0])[:, 0, first_cols[0]])
         load_pair(0)
-        nc.sync.dma_start(out=first_q[:, first_cols[1]], in_=q_relu[0][0:P, first_cols[1]])
+        nc.sync.dma_start(out=first_q[:, first_cols[1]], in_=tokens(q_relu[0])[:, 0, first_cols[1]])
         for g in range(1, H // 2):
             load_pair(g)
         load_batch("keys", keys, 0)
-        load("q", 0, q_relu[0], 1, 1)
+        load("q", 0, tokens(q_relu[0]), 1, 1)
         for first in (0, 2, 4, 6):
-            load("w", 0, Wv, first, 2)
-        load("q", 0, q_relu[0], 2, 2)
+            load("w", 0, Wv.rearrange("(t p) k -> p t k", p=P), first, 2)
+        load("q", 0, tokens(q_relu[0]), 2, 2)
         for tt in range(0, TT, X_TILES):
             for b in range(B):
                 nc.sync.dma_start(
                     out=x_v[:, b * TT + tt : b * TT + tt + X_TILES, :],
-                    in_=queries[b][tt * P : (tt + X_TILES) * P, :].rearrange("(t p) k -> p t k", p=P),
+                    in_=tokens(queries[b])[:, tt : tt + X_TILES, :],
                 )
         load_batch("keys", keys, 1)
         nc.sync.dma_start(out=gamma_b[:], in_=ln_gamma.partition_broadcast(P))
@@ -446,8 +454,8 @@ def tile_multiheadattentionlayer_pa_kernel(
                 tiles["nbias", k] = nbias
 
         def exponentials(j):
-            if j % 4 == 0:
-                tiles["rowsum", j // 4] = small.tile([P, H], F32, tag="rowsum", name="rowsum")
+            if j % 2 == 0:
+                tiles["rowsum", j // 2] = small.tile([P, 4], F32, tag="rowsum", name="rowsum")
             e2 = e_pool.tile([P, 2 * S], BF16, tag="e", name="e2")
             for hh in range(2):
                 k = 2 * j + hh
@@ -457,7 +465,7 @@ def tile_multiheadattentionlayer_pa_kernel(
                     func=ACT.Exp,
                     bias=tiles["nbias", k][:],
                     scale=-1.0,
-                    accum_out=tiles["rowsum", j // 4][:, k % H : k % H + 1],
+                    accum_out=tiles["rowsum", j // 2][:, k % 4 : k % 4 + 1],
                 )
             tiles["e", j] = e2
 
@@ -474,20 +482,24 @@ def tile_multiheadattentionlayer_pa_kernel(
                 ("ebank", j), as_blocks(eg_w[:, (j % 2) * 512 : (j % 2 + 1) * 512]), False
             )
 
-        def quantise_e(n):
-            e_codes = ec_pool.tile([P, 512], U32, tag="ec", name="e_codes", align_bytes=64)
-            e_scales = ec_pool.tile([P, 512], U8, tag="es", name="e_scales", align_bytes=64)
+        def quantise_e(n, heads=(0, 1, 2, 3)):
+            if 0 in heads:
+                tiles["ec", n] = ec_pool.tile([P, 512], U32, tag="ec", name="e_codes", align_bytes=64)
+                tiles["es", n] = ec_pool.tile([P, 512], U8, tag="es", name="e_scales", align_bytes=64)
+            cols = slice(heads[0] * P, (heads[-1] + 1) * P)
             nc.vector.quantize_mx(
-                out=e_codes[:].bitcast(FP8X4), scales=e_scales[:], in_=tiles["eg", n][:]
+                out=tiles["ec", n][:, cols].bitcast(FP8X4),
+                scales=tiles["es", n][:, cols],
+                in_=tiles["eg", n][:, heads[0] * S : (heads[-1] + 1) * S],
             )
-            tiles["ec", n] = e_codes
-            tiles["es", n] = e_scales
 
-        def e_times_v(n):
+        def e_times_v(n, heads=(0, 1, 2, 3)):
             b = n // (2 * TT)
             need(("v", b, n % 2))
-            o_bank = o_psum.tile([P, 512], F32, tag="o", name="o_bank")
-            for h4 in range(4):
+            if 0 in heads:
+                tiles["o", n] = o_psum.tile([P, 512], F32, tag="o", name="o_bank")
+            o_bank = tiles["o", n]
+            for h4 in heads:
                 h = (n % 2) * 4 + h4
                 ec = slice(h4 * P, (h4 + 1) * P)
                 vc = slice((b * H + h) * P, (b * H + h + 1) * P)
@@ -500,39 +512,38 @@ def tile_multiheadattentionlayer_pa_kernel(
                     start=True,
                     stop=True,
                 )
-            tiles["o", n] = o_bank
 
-        def reciprocals(m):
-            rinv = small.tile([P, H], F32, tag="rinv", name="rinv")
-            nc.vector.reciprocal(out=rinv[:], in_=tiles["rowsum", m][:])
-            tiles["rinv", m] = rinv
+        def reciprocals(n):
+            rinv = small.tile([P, 4], F32, tag="rinv", name="rinv")
+            nc.vector.reciprocal(out=rinv[:], in_=tiles["rowsum", n][:])
+            tiles["rinv", n] = rinv
 
-        def masked_reciprocals(m):
-            it = m % TT
+        def masked_reciprocals(n):
+            it = (n // 2) % TT
             need(("mask", 0, it))
             need(("mask", 1, it))
-            r = small.tile([P, H], F32, tag="r", name="r")
+            r = small.tile([P, 4], F32, tag="r", name="r")
             nc.vector.scalar_tensor_tensor(
                 out=r[:].rearrange("p (a c) -> p a c", c=B),
-                in0=msk[:, it * B : (it + 1) * B].unsqueeze(1).to_broadcast([P, H // B, B]),
+                in0=msk[:, it * B : (it + 1) * B].unsqueeze(1).to_broadcast([P, 4 // B, B]),
                 scalar=0.0,
-                in1=tiles["rinv", m][:].rearrange("p (a c) -> p a c", c=B),
+                in1=tiles["rinv", n][:].rearrange("p (a c) -> p a c", c=B),
                 op0=ALU.not_equal,
                 op1=ALU.mult,
             )
-            tiles["r", m] = r
+            tiles["r", n] = r
 
-        def residual(n):
+        def residual(n, heads=(0, 1, 2, 3)):
             m = n // 2
             if n % 2 == 0:
                 tiles["y", m] = y_pool.tile([P, D], F32, tag="y", name="y")
                 tiles["ysum", m] = small.tile([P, H], F32, tag="ysum", name="ysum")
-            for h4 in range(4):
+            for h4 in heads:
                 h = (n % 2) * 4 + h4
                 nc.vector.scalar_tensor_tensor(
                     out=tiles["y", m][:, h * DH : (h + 1) * DH],
                     in0=tiles["o", n][:, h4 * P : (h4 + 1) * P],
-                    scalar=tiles["r", m][:, h : h + 1],
+                    scalar=tiles["r", n][:, h4 : h4 + 1],
                     in1=x_v[:, m, h * DH : (h + 1) * DH],
                     op0=ALU.mult,
                     op1=ALU.add,
@@ -575,13 +586,12 @@ def tile_multiheadattentionlayer_pa_kernel(
             nc.gpsimd.tensor_tensor(out=rstd[:], in0=veps[:], in1=neg_half[:], op=ALU.pow)
             tiles["rstd", m] = rstd
 
-        def half_statistics(n):
-            m = n // 2
-            if n % 2 == 0:
-                tiles["stats", m] = small.tile([P, 12], F32, tag="stats", name="stats")
+        def part_statistics(m, part):
+            if part == 0:
+                tiles["stats", m] = small.tile([P, 6 * len(STAT_PARTS)], F32, tag="stats", name="stats")
             nc.vector.bn_stats(
-                out=tiles["stats", m][:, (n % 2) * 6 : (n % 2 + 1) * 6],
-                in_=tiles["y", m][:, (n % 2) * 512 : (n % 2 + 1) * 512],
+                out=tiles["stats", m][:, part * 6 : (part + 1) * 6],
+                in_=tiles["y", m][:, STAT_PARTS[part][0] * DH : STAT_PARTS[part][1] * DH],
             )
 
         def aggregate(m):
@@ -604,7 +614,7 @@ def tile_multiheadattentionlayer_pa_kernel(
         QUARTERS = tuple(slice(c, c + 256) for c in range(0, D, 256))
 
         def store(m, cols, queue=nc.sync):
-            rows = out[m // TT, (m % TT) * P : (m % TT + 1) * P, :]
+            rows = tokens(out[m // TT])[:, m % TT, :]
             queue.dma_start(out=rows[:, cols], in_=tiles["res", m][:, cols])
 
         def normalise_gpsimd(m, parts):
@@ -668,10 +678,17 @@ def tile_multiheadattentionlayer_pa_kernel(
             plan.setdefault(step, []).append((call, args))
 
         last = UNITS - 1
-        for m in range(UNITS):
-            among[4 * m + 4] = [(reciprocals, (m,))]
-            at(ev_step(2 * m) + 1, masked_reciprocals, m)
         for n in range(HALVES):
+            among[2 * n + RECIP] = [(reciprocals, (n,))]
+            at(max(2 * n + MASKED, ev_step(n) - R_EARLY), masked_reciprocals, n)
+        for n in range(HALVES):
+            if n == HALVES - 1:
+                for i, pair in enumerate(((0, 1), (2, 3))):
+                    at(2 * n + 2 + i, quantise_e, n, pair)
+                    at(2 * n + 2 + i, e_times_v, n, pair)
+                for i, pair in enumerate(((0, 1), (2, 3))):
+                    at(2 * n + 3 + i, residual, n, pair)
+                continue
             at(2 * n + 3, quantise_e, n)
             at(ev_step(n), e_times_v, n)
             at(ev_step(n) + 1, residual, n)
@@ -684,12 +701,13 @@ def tile_multiheadattentionlayer_pa_kernel(
             elif m < last:
                 at(s, mean, m)
                 at(s + 1, row_statistics, m)
-                at(s + 2, center, m, halves[:1])
+                at(s + CENTER, center, m, halves[:1])
                 at(s + 2, normalise_gpsimd, m, halves[1:])
                 at(s + 4, scale, m, halves[:1])
             else:
-                at(s - 2, half_statistics, 2 * m)
-                at(s - 1, half_statistics, 2 * m + 1)
+                at(s - 2, part_statistics, m, 0)
+                at(s - 2, part_statistics, m, 1)
+                at(s - 1, part_statistics, m, 2)
                 at(s - 1, warm_sqrt)
                 at(s - 1, aggregate, m)
                 at(s, center, m, halves)

@@ -33,9 +33,10 @@ STAT_PARTS = ((0, 4), (4, 6), (6, 8))
 AHEAD = 1
 SNEG_BUFS = 2 * AHEAD + 4
 VECTOR_UNITS = 2
-EVERY = {("keys", 0): 2, ("keys", 1): 3, ("w", 0): 4, ("relu", 0): 100, ("relu", 1): 3, ("v", 0): 100, ("v", 1): 3}
-SCALAR_HEADS = (("pair", 1), ("pair", 3), ("q", 0, 1), ("q", 0, 3), ("k", 1, 0), ("k", 1, 1), ("k", 1, 3), ("q", 1, 1), ("q", 1, 3))
+VECTORS = {("heads", 0): (2,), ("heads", 1): (2,), ("keys", 0): (1, 3), ("keys", 1): (2,), ("w", 0): (3,), ("relu", 0): (), ("relu", 1): (1, 3), ("v", 0): (), ("v", 1): (2,)}
 SCALAR_MASKS = 0
+K_CHUNKS = ((1, 1), (2, 2))
+LATE = 2
 CENTER = 1
 RECIP = 2
 MASKED = 2
@@ -107,8 +108,9 @@ def tile_multiheadattentionlayer_pa_kernel(
             return rows.rearrange("(p t) k -> p t k", t=TT)
 
         def load(name, b, tiled, first, count):
-            raw = raw_pool.tile([P, 2 * D], BF16, tag="raw", name="raw")
-            raw_v = raw[:].rearrange("p (a k) -> p a k", a=2)
+            wide = 4 if count == 4 else 2
+            raw = raw_pool.tile([P, wide * D], BF16, tag="raw" + str(wide), name="raw", bufs=8 if wide == 2 else 3)
+            raw_v = raw[:].rearrange("p (a k) -> p a k", a=wide)
             nc.sync.dma_start(
                 out=raw_v[:, 0:count, :],
                 in_=tiled[:, first : first + count, :],
@@ -117,24 +119,27 @@ def tile_multiheadattentionlayer_pa_kernel(
                 raws[name, b, first + a] = raw[:, a * D : (a + 1) * D]
 
         def load_batch(name, src, b):
-            for first in (0, 2):
-                load(name, b, tokens(src[b]), first, 2)
+            count = LATE if b == 1 else 2
+            for first in range(0, TT, count):
+                load(name, b, tokens(src[b]), first, count)
 
-        def load_pair(g):
-            raw = raw_pool.tile([P, TT * 2 * DH], BF16, tag="rawk", name="rawk", bufs=4)
+        def load_pair(g, count):
+            raw = raw_pool.tile([P, TT * count * 2 * DH], BF16, tag="rawk" + str(g), name="rawk", bufs=1)
+            raw_v = raw[:].rearrange("p (t k) -> p t k", t=TT)
             nc.sync.dma_start(
-                out=raw[:].rearrange("p (t k) -> p t k", t=TT),
-                in_=tokens(k_relu[0])[:, :, g * 2 * DH : (g + 1) * 2 * DH],
+                out=raw_v,
+                in_=tokens(k_relu[0])[:, :, g * 2 * DH : (g + count) * 2 * DH],
             )
-            raws["k", 0, "pair", g] = raw
+            for i in range(count):
+                raws["k", 0, "pair", g + i] = raw_v[:, :, i * 2 * DH : (i + 1) * 2 * DH]
 
         first_q = raw_pool.tile([P, D], BF16, tag="rawq", name="rawq", bufs=1)
         first_cols = (slice(0, 2 * DH), slice(2 * DH, D))
         nc.sync.dma_start(out=first_q[:, first_cols[0]], in_=tokens(q_relu[0])[:, 0, first_cols[0]])
-        load_pair(0)
+        load_pair(0, 1)
         nc.sync.dma_start(out=first_q[:, first_cols[1]], in_=tokens(q_relu[0])[:, 0, first_cols[1]])
-        for g in range(1, H // 2):
-            load_pair(g)
+        for first, count in K_CHUNKS:
+            load_pair(first, count)
         load_batch("keys", keys, 0)
         load("q", 0, tokens(q_relu[0]), 1, 1)
         for first in (0, 2, 4, 6):
@@ -155,12 +160,8 @@ def tile_multiheadattentionlayer_pa_kernel(
         tiles = {}
         done = set()
 
-        turn = {}
-
-        def vectors_turn(b, kind):
-            key = (kind, b)
-            turn[key] = turn.get(key, 0) + 1
-            return turn[key] % EVERY[key] == 0
+        def vectors(kind, b, i):
+            return i % 4 in VECTORS[kind, b]
 
         def word_transposes(key, words):
             bank = bank_psum.tile([P, 512], F32, tag="bank", name="bank")
@@ -190,11 +191,10 @@ def tile_multiheadattentionlayer_pa_kernel(
             bank = bank_psum.tile([P, 1024], BF16, tag="bank", name="bank_p")
             for hh in range(2):
                 for tt in range(TT):
-                    first = tt * 2 * DH + hh * DH
                     block = (hh * TT + tt) * P
                     nc.tensor.transpose(
                         bank[:, block : block + P],
-                        raws["k", 0, "pair", g][:, first : first + DH],
+                        raws["k", 0, "pair", g][:, tt, hh * DH : (hh + 1) * DH],
                         ident_b[:],
                     )
             tiles["pair", g] = bank
@@ -205,7 +205,7 @@ def tile_multiheadattentionlayer_pa_kernel(
             if g == 0:
                 nc.vector.tensor_copy(out=dst[:, 0, :], in_=src[:, 0, :])
                 nc.scalar.copy(out=dst[:, 1, :], in_=src[:, 1, :])
-            elif ("pair", g) not in SCALAR_HEADS:
+            elif vectors("heads", 0, g):
                 nc.vector.tensor_copy(out=dst, in_=src)
             else:
                 nc.scalar.copy(out=dst, in_=src)
@@ -230,7 +230,7 @@ def tile_multiheadattentionlayer_pa_kernel(
         def heads_back(name, b, tt):
             dst = heads_T[name][:, b, :, tt * P : (tt + 1) * P]
             src = tiles[name, b, tt][:].rearrange("p (h r) -> p h r", h=H)
-            if (name, b, tt) not in SCALAR_HEADS:
+            if vectors("heads", b, tt):
                 nc.vector.tensor_copy(out=dst, in_=src)
             else:
                 nc.scalar.copy(out=dst, in_=src)
@@ -243,7 +243,7 @@ def tile_multiheadattentionlayer_pa_kernel(
             if tt == 0:
                 tiles["kg", b] = grp_pool.tile([P, 4096], BF16, tag="grp", name="kg", align_bytes=64)
             kg_v = tiles["kg", b][:].bitcast(F32).rearrange("p (g s u) -> p g s u", g=2, u=2)
-            copy_interleaved((name, b, tt), kg_v[:, :, tt * P : (tt + 1) * P, :], vectors_turn(b, "keys"))
+            copy_interleaved((name, b, tt), kg_v[:, :, tt * P : (tt + 1) * P, :], vectors("keys", b, tt))
 
         def quantise_keys(b, c):
             cols = slice(b * 1024 + c * S, b * 1024 + (c + 1) * S)
@@ -262,7 +262,7 @@ def tile_multiheadattentionlayer_pa_kernel(
                 )
             wg_w = tiles["wg", ct // 4][:].bitcast(F32)
             copy_interleaved(
-                (name, b, ct), as_blocks(wg_w[:, (ct % 4) * 512 : (ct % 4 + 1) * 512]), vectors_turn(b, "w")
+                (name, b, ct), as_blocks(wg_w[:, (ct % 4) * 512 : (ct % 4 + 1) * 512]), vectors("w", b, ct)
             )
 
         def quantise_w(half):
@@ -300,7 +300,7 @@ def tile_multiheadattentionlayer_pa_kernel(
             if h % 2 == 0:
                 tiles["vT", b, h // 2] = vt_pool.tile([P, 2 * S], BF16, tag="vt", name="vT")
             dst = tiles["vT", b, h // 2][:, (h % 2) * S : (h % 2 + 1) * S]
-            if not vectors_turn(b, "relu"):
+            if not vectors("relu", b, h):
                 nc.scalar.activation(
                     out=dst, in_=tiles["acc", b, h][:], func=ACT.Relu, bias=bvT[:, h : h + 1], scale=1.0
                 )
@@ -325,7 +325,7 @@ def tile_multiheadattentionlayer_pa_kernel(
                 )
             vg_w = tiles["vg", b, g // 2][:].bitcast(F32)
             copy_interleaved(
-                ("vbank", b, g), as_blocks(vg_w[:, (g % 2) * 512 : (g % 2 + 1) * 512]), vectors_turn(b, "v")
+                ("vbank", b, g), as_blocks(vg_w[:, (g % 2) * 512 : (g % 2 + 1) * 512]), vectors("v", b, g)
             )
 
         def quantise_v(b, half):

import math
from contextlib import ExitStack

import concourse.mybir as mybir
from concourse.masks import make_identity

F32 = mybir.dt.float32
BF16 = mybir.dt.bfloat16
U32 = mybir.dt.uint32
U8 = mybir.dt.uint8
FP8X4 = mybir.dt.float8_e4m3fn_x4
ACT = mybir.ActivationFunctionType
ALU = mybir.AluOpType

P = 128
B = 2
S = 512
D = 1024
H = 8
DH = D // H
TT = S // P
SCALE = 1.0 / math.sqrt(DH)
LN_EPS = 1e-8

UNITS = B * TT
HALVES = UNITS * 2
PAIRS = UNITS * 4
JOBS_PER_STEP = 2
EV_FIRST = 7
EV_SECOND = 19
JOBS_FIRST = 6
STAT_PARTS = ((0, 4), (4, 6), (6, 8))
AHEAD = 1
SNEG_BUFS = 2 * AHEAD + 4
VECTOR_UNITS = 2
VECTORS = {("heads", 0): (2,), ("heads", 1): (2,), ("keys", 0): (1, 3), ("keys", 1): (2,), ("w", 0): (3,), ("relu", 0): (), ("relu", 1): (1, 3), ("v", 0): (), ("v", 1): (2,)}
SCALAR_MASKS = 0
K_CHUNKS = ((1, 1), (2, 2))
LATE = 2
CENTER = 1
RECIP = 2
MASKED = 2
R_EARLY = 0
X_TILES = 2
MASKS_AT = (0, 0, 0)
BIAS_LATER = 0
LEAD = 1

FLOPS = 2 * B * S * D * D + 2 * 2 * B * H * S * S * DH


def tile_multiheadattentionlayer_pa_kernel(
    tc, q_relu, k_relu, keys, Wv, bv, queries, ln_gamma, ln_beta, out
):
    nc = tc.nc
    with ExitStack() as ctx:
        ctx.enter_context(tc.manual_schedule())
        const = ctx.enter_context(tc.tile_pool(name="const", bufs=1))
        keep = ctx.enter_context(tc.tile_pool(name="keep", bufs=1))
        raw_pool = ctx.enter_context(tc.tile_pool(name="raw", bufs=8))
        grp_pool = ctx.enter_context(tc.tile_pool(name="grp", bufs=2))
        vt_pool = ctx.enter_context(tc.tile_pool(name="vt", bufs=3))
        s_pool = ctx.enter_context(tc.tile_pool(name="s", bufs=SNEG_BUFS))
        e_pool = ctx.enter_context(tc.tile_pool(name="e", bufs=3))
        eg_pool = ctx.enter_context(tc.tile_pool(name="eg", bufs=3))
        ec_pool = ctx.enter_context(tc.tile_pool(name="ec", bufs=6))
        y_pool = ctx.enter_context(tc.tile_pool(name="y", bufs=3))
        junk_pool = ctx.enter_context(tc.tile_pool(name="junk", bufs=2))
        small = ctx.enter_context(tc.tile_pool(name="small", bufs=12))
        bank_psum = ctx.enter_context(tc.psum_pool(name="bank", bufs=4))
        s_psum = ctx.enter_context(tc.psum_pool(name="sc", bufs=3))
        o_psum = ctx.enter_context(tc.psum_pool(name="o", bufs=1))

        ident_b = const.tile([P, P], BF16)
        make_identity(nc, ident_b[:])
        ident_w = const.tile([P, P], F32)
        make_identity(nc, ident_w[:])
        neg_half = const.tile([P, 1], F32)
        nc.vector.memset(neg_half[:], -0.5)
        warm = const.tile([P, 1], F32)
        nc.scalar.activation(out=warm[:], in_=neg_half[:], func=ACT.Exp)
        bv_rows = const.tile([P, P], BF16)
        nc.vector.memset(bv_rows[:], 0.0)
        nc.scalar.dma_start(out=bv_rows[0:H, :], in_=bv.rearrange("(t c) -> t c", c=P))

        w_codes = keep.tile([P, 2048], U32, align_bytes=64)
        w_scales = keep.tile([P, 2048], U8, align_bytes=64)
        k_codes = keep.tile([P, 2048], U32, align_bytes=64)
        k_scales = keep.tile([P, 2048], U8, align_bytes=64)
        v_codes = keep.tile([P, 2048], U32, align_bytes=64)
        v_scales = keep.tile([P, 2048], U8, align_bytes=64)
        qT = keep.tile([P, B * H * S], BF16)
        kT = keep.tile([P, B * H * S], BF16)
        x_sb = keep.tile([P, B * TT * D], BF16)
        gamma_b = keep.tile([P, D], BF16)
        beta_b = keep.tile([P, D], BF16)
        msk = keep.tile([P, TT * B], F32)
        bvT = keep.tile([P, H], F32)
        heads_T = {
            "q": qT[:].rearrange("p (b h s) -> p b h s", b=B, h=H),
            "k": kT[:].rearrange("p (b h s) -> p b h s", b=B, h=H),
        }
        x_v = x_sb[:].rearrange("p (t k) -> p t k", t=B * TT)

        raws = {}

        def tokens(rows):
            return rows.rearrange("(p t) k -> p t k", t=TT)

        def load(name, b, tiled, first, count):
            wide = 4 if count == 4 else 2
            raw = raw_pool.tile([P, wide * D], BF16, tag="raw" + str(wide), name="raw", bufs=8 if wide == 2 else 3)
            raw_v = raw[:].rearrange("p (a k) -> p a k", a=wide)
            nc.sync.dma_start(
                out=raw_v[:, 0:count, :],
                in_=tiled[:, first : first + count, :],
            )
            for a in range(count):
                raws[name, b, first + a] = raw[:, a * D : (a + 1) * D]

        def load_batch(name, src, b):
            count = LATE if b == 1 else 2
            for first in range(0, TT, count):
                load(name, b, tokens(src[b]), first, count)

        def load_pair(g, count):
            raw = raw_pool.tile([P, TT * count * 2 * DH], BF16, tag="rawk" + str(g), name="rawk", bufs=1)
            raw_v = raw[:].rearrange("p (t k) -> p t k", t=TT)
            nc.sync.dma_start(
                out=raw_v,
                in_=tokens(k_relu[0])[:, :, g * 2 * DH : (g + count) * 2 * DH],
            )
            for i in range(count):
                raws["k", 0, "pair", g + i] = raw_v[:, :, i * 2 * DH : (i + 1) * 2 * DH]

        first_q = raw_pool.tile([P, D], BF16, tag="rawq", name="rawq", bufs=1)
        first_cols = (slice(0, 2 * DH), slice(2 * DH, D))
        nc.sync.dma_start(out=first_q[:, first_cols[0]], in_=tokens(q_relu[0])[:, 0, first_cols[0]])
        load_pair(0, 1)
        nc.sync.dma_start(out=first_q[:, first_cols[1]], in_=tokens(q_relu[0])[:, 0, first_cols[1]])
        for first, count in K_CHUNKS:
            load_pair(first, count)
        load_batch("keys", keys, 0)
        load("q", 0, tokens(q_relu[0]), 1, 1)
        for first in (0, 2, 4, 6):
            load("w", 0, Wv.rearrange("(t p) k -> p t k", p=P), first, 2)
        load("q", 0, tokens(q_relu[0]), 2, 2)
        for tt in range(0, TT, X_TILES):
            for b in range(B):
                nc.sync.dma_start(
                    out=x_v[:, b * TT + tt : b * TT + tt + X_TILES, :],
                    in_=tokens(queries[b])[:, tt : tt + X_TILES, :],
                )
        load_batch("keys", keys, 1)
        nc.sync.dma_start(out=gamma_b[:], in_=ln_gamma.partition_broadcast(P))
        nc.sync.dma_start(out=beta_b[:], in_=ln_beta.partition_broadcast(P))
        load_batch("k", k_relu, 1)
        load_batch("q", q_relu, 1)

        tiles = {}
        done = set()

        def vectors(kind, b, i):
            return i % 4 in VECTORS[kind, b]

        def word_transposes(key, words):
            bank = bank_psum.tile([P, 512], F32, tag="bank", name="bank")
            for k in range(4):
                cols = slice(k * P, (k + 1) * P)
                nc.tensor.transpose(bank[:, cols], words[:, cols], ident_w[:])
            tiles[key] = bank

        def copy_interleaved(key, grouped, on_vector):
            src = tiles[key][:].rearrange("p (a u r) -> p a r u", a=2, u=2)
            if on_vector:
                nc.vector.tensor_copy(out=grouped, in_=src)
            else:
                nc.scalar.copy(out=grouped, in_=src)

        def as_blocks(words):
            return words.rearrange("p (a r u) -> p a r u", a=2, u=2)

        def heads_front(name, b, tt):
            bank = bank_psum.tile([P, 1024], BF16, tag="bank", name="bank_b")
            for h in range(H):
                cols = slice(h * DH, (h + 1) * DH)
                nc.tensor.transpose(bank[:, cols], raws[name, b, tt][:, cols], ident_b[:])
            tiles[name, b, tt] = bank

        def pair_front(g):
            bank = bank_psum.tile([P, 1024], BF16, tag="bank", name="bank_p")
            for hh in range(2):
                for tt in range(TT):
                    block = (hh * TT + tt) * P
                    nc.tensor.transpose(
                        bank[:, block : block + P],
                        raws["k", 0, "pair", g][:, tt, hh * DH : (hh + 1) * DH],
                        ident_b[:],
                    )
            tiles["pair", g] = bank

        def pair_back(g):
            dst = heads_T["k"][:, 0, 2 * g : 2 * g + 2, :]
            src = tiles["pair", g][:].rearrange("p (h r) -> p h r", h=2)
            if g == 0:
                nc.vector.tensor_copy(out=dst[:, 0, :], in_=src[:, 0, :])
                nc.scalar.copy(out=dst[:, 1, :], in_=src[:, 1, :])
            elif vectors("heads", 0, g):
                nc.vector.tensor_copy(out=dst, in_=src)
            else:
                nc.scalar.copy(out=dst, in_=src)
            done.add(("k", 0, "pair", g))

        def first_front(part):
            cols = first_cols[part]
            bank = bank_psum.tile([P, 1024], BF16, tag="bank", name="bank_q")
            for first in range(cols.start, cols.stop, DH):
                nc.tensor.transpose(bank[:, first : first + DH], first_q[:, first : first + DH], ident_b[:])
            tiles["first", part] = bank

        def first_back(part):
            cols = first_cols[part]
            heads = slice(cols.start // DH, cols.stop // DH)
            nc.vector.tensor_copy(
                out=heads_T["q"][:, 0, heads, 0:P],
                in_=tiles["first", part][:, cols].rearrange("p (h r) -> p h r", r=P),
            )
            done.add(("q", 0, 0, part))

        def heads_back(name, b, tt):
            dst = heads_T[name][:, b, :, tt * P : (tt + 1) * P]
            src = tiles[name, b, tt][:].rearrange("p (h r) -> p h r", h=H)
            if vectors("heads", b, tt):
                nc.vector.tensor_copy(out=dst, in_=src)
            else:
                nc.scalar.copy(out=dst, in_=src)
            done.add((name, b, tt))

        def rows_front(name, b, t):
            word_transposes((name, b, t), raws[name, b, t].bitcast(F32))

        def keys_back(name, b, tt):
            if tt == 0:
                tiles["kg", b] = grp_pool.tile([P, 4096], BF16, tag="grp", name="kg", align_bytes=64)
            kg_v = tiles["kg", b][:].bitcast(F32).rearrange("p (g s u) -> p g s u", g=2, u=2)
            copy_interleaved((name, b, tt), kg_v[:, :, tt * P : (tt + 1) * P, :], vectors("keys", b, tt))

        def quantise_keys(b, c):
            cols = slice(b * 1024 + c * S, b * 1024 + (c + 1) * S)
            nc.vector.quantize_mx(
                out=k_codes[:, cols].bitcast(FP8X4),
                scales=k_scales[:, cols],
                in_=tiles["kg", b][:, c * 2048 : (c + 1) * 2048],
            )
            if c == 1:
                done.add(("keys", b))

        def w_back(name, b, ct):
            if ct % 4 == 0:
                tiles["wg", ct // 4] = grp_pool.tile(
                    [P, 4096], BF16, tag="grp", name="wg", align_bytes=64
                )
            wg_w = tiles["wg", ct // 4][:].bitcast(F32)
            copy_interleaved(
                (name, b, ct), as_blocks(wg_w[:, (ct % 4) * 512 : (ct % 4 + 1) * 512]), vectors("w", b, ct)
            )

        def quantise_w(half):
            cols = slice(half * 1024, (half + 1) * 1024)
            nc.vector.quantize_mx(
                out=w_codes[:, cols].bitcast(FP8X4), scales=w_scales[:, cols], in_=tiles["wg", half][:]
            )
            done.add(("w", half))

        def bias_front():
            bv_bank = bank_psum.tile([P, 1024], BF16, tag="bank", name="bv_bank")
            nc.tensor.transpose(bv_bank[:, 0:P], bv_rows[:], ident_b[:])
            tiles["bv"] = bv_bank

        def bias_back():
            nc.vector.tensor_copy(out=bvT[:], in_=tiles["bv"][:, 0:H])

        def project_front(b, h):
            acc = bank_psum.tile([P, S], F32, tag="bank", name="acc")
            for c in range(2):
                wc = slice(h * 256 + c * P, h * 256 + (c + 1) * P)
                kc = slice(b * 1024 + c * S, b * 1024 + (c + 1) * S)
                nc.tensor.matmul_mx(
                    out=acc[:],
                    lhsT=w_codes[:, wc].bitcast(FP8X4),
                    lhsT_scale=w_scales[:, wc],
                    rhs=k_codes[:, kc].bitcast(FP8X4),
                    rhs_scale=k_scales[:, kc],
                    start=(c == 0),
                    stop=(c == 1),
                )
            tiles["acc", b, h] = acc

        def project_back(b, h):
            if h % 2 == 0:
                tiles["vT", b, h // 2] = vt_pool.tile([P, 2 * S], BF16, tag="vt", name="vT")
            dst = tiles["vT", b, h // 2][:, (h % 2) * S : (h % 2 + 1) * S]
            if not vectors("relu", b, h):
                nc.scalar.activation(
                    out=dst, in_=tiles["acc", b, h][:], func=ACT.Relu, bias=bvT[:, h : h + 1], scale=1.0
                )
            else:
                nc.vector.tensor_scalar(
                    out=dst,
                    in0=tiles["acc", b, h][:],
                    scalar1=bvT[:, h : h + 1],
                    scalar2=0.0,
                    op0=ALU.add,
                    op1=ALU.max,
                )
            done.add(("vT", b, h))

        def v_front(b, g):
            word_transposes(("vbank", b, g), tiles["vT", b, g][:].bitcast(F32))

        def v_back(b, g):
            if g % 2 == 0:
                tiles["vg", b, g // 2] = eg_pool.tile(
                    [P, 2048], BF16, tag="eg", name="vg", align_bytes=64
                )
            vg_w = tiles["vg", b, g // 2][:].bitcast(F32)
            copy_interleaved(
                ("vbank", b, g), as_blocks(vg_w[:, (g % 2) * 512 : (g % 2 + 1) * 512]), vectors("v", b, g)
            )

        def quantise_v(b, half):
            cols = slice((b * 2 + half) * 512, (b * 2 + half + 1) * 512)
            nc.vector.quantize_mx(
                out=v_codes[:, cols].bitcast(FP8X4),
                scales=v_scales[:, cols],
                in_=tiles["vg", b, half][:],
            )
            done.add(("v", b, half))

        def mask_rows(b, tt):
            mjunk = junk_pool.tile([P, D], BF16, tag="mjunk", name="mjunk")
            anything = msk[:, tt * B + b : tt * B + b + 1]
            if tt >= TT - SCALAR_MASKS:
                nc.scalar.activation(
                    out=mjunk[:], in_=x_v[:, b * TT + tt, :], func=ACT.Abs, accum_out=anything
                )
            else:
                nc.vector.tensor_scalar(
                    out=mjunk[:],
                    in0=x_v[:, b * TT + tt, :],
                    scalar1=0.0,
                    scalar2=None,
                    op0=ALU.not_equal,
                    op1=ALU.max,
                    accum_out=anything,
                )
            done.add(("mask", b, tt))

        def merged(copies, others):
            out = []
            for i, job in enumerate(copies):
                out.append(job)
                for k in range(len(others)):
                    if (k + 1) * len(copies) // (len(others) + 1) == i:
                        out.append(others[k])
            return out

        def only(call, *args):
            return (None, call, args, ())

        mask_jobs = [only(mask_rows, bb, tt) for tt in range(TT) for bb in range(B)]
        jobs = []
        for b in range(B):
            if b == 0:
                jobs.append((first_front, first_back, (0,), ()))
                jobs.append((pair_front, pair_back, (0,), ()))
                jobs.append((first_front, first_back, (1,), ()))
                jobs.extend([(pair_front, pair_back, (g,), ()) for g in range(1, H // 2)])
            else:
                jobs.append((heads_front, heads_back, ("q", b, 0), ()))
                jobs.extend([(heads_front, heads_back, ("k", b, tt), ()) for tt in range(TT)])
            later_q = [(heads_front, heads_back, ("q", b, tt), ()) for tt in range(1, TT)]
            jobs.extend([(rows_front, keys_back, ("keys", b, tt), ()) for tt in range(TT)])
            quantised = [only(quantise_keys, b, c) for c in range(2)]
            projected = [
                (project_front, project_back, (b, h), (("keys", b), ("w", h // 4))) for h in range(H)
            ]
            turned = [(v_front, v_back, (b, g), (("vT", b, 2 * g + 1),)) for g in range(4)]
            if b == 0:
                weights = [(rows_front, w_back, ("w", 0, ct), ()) for ct in range(H)]
                bias_at = len(jobs) + BIAS_LATER
                m1, m2, m3 = MASKS_AT
                jobs.extend(merged(later_q[:1] + weights[:4], quantised + mask_jobs[:m1]))
                jobs.extend(merged(weights[4:], [only(quantise_w, 0)] + mask_jobs[m1:m2]))
                jobs.extend(merged(later_q[1:], mask_jobs[m2:m3]) + [only(quantise_w, 1)])
                jobs.insert(bias_at, (bias_front, bias_back, (), ()))
                jobs.extend(merged(projected[:6], mask_jobs[m3:8]))
            else:
                jobs.extend(merged(later_q, quantised))
                jobs.extend(projected[:6])
            jobs.extend(turned[:2] + projected[6:] + [only(quantise_v, b, 0)] + turned[2:] + [only(quantise_v, b, 1)])
        issued = {"front": 0, "back": 0}

        def advance():
            if issued["back"] == len(jobs):
                return
            while issued["front"] < min(issued["back"] + LEAD + 1, len(jobs)):
                front, back, args, before = jobs[issued["front"]]
                if not all(key in done for key in before):
                    break
                if front is not None:
                    front(*args)
                issued["front"] += 1
            front, back, args, before = jobs[issued["back"]]
            back(*args)
            issued["back"] += 1

        def need(key):
            while key not in done:
                advance()

        def scores(j):
            for k in (2 * j, 2 * j + 1):
                b, it, h = k // (H * TT), (k // H) % TT, k % H
                need(("k", b, "pair", h // 2) if b == 0 else ("k", b, TT - 1))
                need(("q", b, it) if (b, it) != (0, 0) else ("q", 0, 0, min(h // 2, 1)))
                s_bank = s_psum.tile([P, S], F32, tag="s", name="s_bank")
                nc.tensor.matmul(
                    out=s_bank[:],
                    lhsT=heads_T["q"][:, b, h, it * P : (it + 1) * P],
                    rhs=heads_T["k"][:, b, h, :],
                    start=True,
                    stop=True,
                )
                tiles["s", k] = s_bank

        def row_max(j, between=()):
            for k in (2 * j, 2 * j + 1):
                if k % 2 == 1:
                    for call, args in between:
                        call(*args)
                sneg = s_pool.tile([P, S], F32, tag="sneg", name="sneg")
                nbias = small.tile([P, 1], F32, tag="nbias", name="nbias", bufs=SNEG_BUFS)
                nc.vector.tensor_scalar(
                    out=sneg[:],
                    in0=tiles["s", k][:],
                    scalar1=-SCALE,
                    scalar2=None,
                    op0=ALU.mult,
                    op1=ALU.min,
                    accum_out=nbias[:],
                )
                tiles["sneg", k] = sneg
                tiles["nbias", k] = nbias

        def exponentials(j):
            if j % 2 == 0:
                tiles["rowsum", j // 2] = small.tile([P, 4], F32, tag="rowsum", name="rowsum")
            e2 = e_pool.tile([P, 2 * S], BF16, tag="e", name="e2")
            for hh in range(2):
                k = 2 * j + hh
                nc.scalar.activation(
                    out=e2[:, hh * S : (hh + 1) * S],
                    in_=tiles["sneg", k][:],
                    func=ACT.Exp,
                    bias=tiles["nbias", k][:],
                    scale=-1.0,
                    accum_out=tiles["rowsum", j // 2][:, k % 4 : k % 4 + 1],
                )
            tiles["e", j] = e2

        def transpose_e(j):
            word_transposes(("ebank", j), tiles["e", j][:].bitcast(F32))

        def copy_e(j):
            if j % 2 == 0:
                tiles["eg", j // 2] = eg_pool.tile(
                    [P, 2048], BF16, tag="eg", name="eg", align_bytes=64
                )
            eg_w = tiles["eg", j // 2][:].bitcast(F32)
            copy_interleaved(
                ("ebank", j), as_blocks(eg_w[:, (j % 2) * 512 : (j % 2 + 1) * 512]), False
            )

        def quantise_e(n, heads=(0, 1, 2, 3)):
            if 0 in heads:
                tiles["ec", n] = ec_pool.tile([P, 512], U32, tag="ec", name="e_codes", align_bytes=64)
                tiles["es", n] = ec_pool.tile([P, 512], U8, tag="es", name="e_scales", align_bytes=64)
            cols = slice(heads[0] * P, (heads[-1] + 1) * P)
            nc.vector.quantize_mx(
                out=tiles["ec", n][:, cols].bitcast(FP8X4),
                scales=tiles["es", n][:, cols],
                in_=tiles["eg", n][:, heads[0] * S : (heads[-1] + 1) * S],
            )

        def e_times_v(n, heads=(0, 1, 2, 3)):
            b = n // (2 * TT)
            need(("v", b, n % 2))
            if 0 in heads:
                tiles["o", n] = o_psum.tile([P, 512], F32, tag="o", name="o_bank")
            o_bank = tiles["o", n]
            for h4 in heads:
                h = (n % 2) * 4 + h4
                ec = slice(h4 * P, (h4 + 1) * P)
                vc = slice((b * H + h) * P, (b * H + h + 1) * P)
                nc.tensor.matmul_mx(
                    out=o_bank[:, ec],
                    lhsT=tiles["ec", n][:, ec].bitcast(FP8X4),
                    lhsT_scale=tiles["es", n][:, ec],
                    rhs=v_codes[:, vc].bitcast(FP8X4),
                    rhs_scale=v_scales[:, vc],
                    start=True,
                    stop=True,
                )

        def reciprocals(n):
            rinv = small.tile([P, 4], F32, tag="rinv", name="rinv")
            nc.vector.reciprocal(out=rinv[:], in_=tiles["rowsum", n][:])
            tiles["rinv", n] = rinv

        def masked_reciprocals(n):
            it = (n // 2) % TT
            need(("mask", 0, it))
            need(("mask", 1, it))
            r = small.tile([P, 4], F32, tag="r", name="r")
            nc.vector.scalar_tensor_tensor(
                out=r[:].rearrange("p (a c) -> p a c", c=B),
                in0=msk[:, it * B : (it + 1) * B].unsqueeze(1).to_broadcast([P, 4 // B, B]),
                scalar=0.0,
                in1=tiles["rinv", n][:].rearrange("p (a c) -> p a c", c=B),
                op0=ALU.not_equal,
                op1=ALU.mult,
            )
            tiles["r", n] = r

        def residual(n, heads=(0, 1, 2, 3)):
            m = n // 2
            if n % 2 == 0:
                tiles["y", m] = y_pool.tile([P, D], F32, tag="y", name="y")
                tiles["ysum", m] = small.tile([P, H], F32, tag="ysum", name="ysum")
            for h4 in heads:
                h = (n % 2) * 4 + h4
                nc.vector.scalar_tensor_tensor(
                    out=tiles["y", m][:, h * DH : (h + 1) * DH],
                    in0=tiles["o", n][:, h4 * P : (h4 + 1) * P],
                    scalar=tiles["r", n][:, h4 : h4 + 1],
                    in1=x_v[:, m, h * DH : (h + 1) * DH],
                    op0=ALU.mult,
                    op1=ALU.add,
                    accum_out=tiles["ysum", m][:, h : h + 1] if m < UNITS - 1 else None,
                )

        def mean(m):
            junk8 = small.tile([P, H], F32, tag="junk8", name="junk8")
            negmu = small.tile([P, 1], F32, tag="negmu", name="negmu")
            nc.vector.tensor_scalar(
                out=junk8[:],
                in0=tiles["ysum", m][:],
                scalar1=-1.0 / D,
                scalar2=None,
                op0=ALU.mult,
                op1=ALU.add,
                accum_out=negmu[:],
            )
            tiles["negmu", m] = negmu

        def row_statistics(m):
            sq = junk_pool.tile([P, D], BF16, tag="sq", name="sq")
            ssq = small.tile([P, 1], F32, tag="ssq", name="ssq")
            nc.scalar.activation(
                out=sq[:],
                in_=tiles["y", m][:],
                func=ACT.Square,
                bias=tiles["negmu", m][:],
                scale=1.0,
                accum_out=ssq[:],
            )
            inverse_deviation(m, ssq[:], 1.0 / D)

        def inverse_deviation(m, squares, factor):
            veps = small.tile([P, 1], F32, tag="veps", name="veps")
            nc.gpsimd.tensor_scalar(
                out=veps[:], in0=squares, scalar1=factor, scalar2=LN_EPS, op0=ALU.mult, op1=ALU.add
            )
            rstd = small.tile([P, 1], F32, tag="rstd", name="rstd")
            nc.gpsimd.tensor_tensor(out=rstd[:], in0=veps[:], in1=neg_half[:], op=ALU.pow)
            tiles["rstd", m] = rstd

        def part_statistics(m, part):
            if part == 0:
                tiles["stats", m] = small.tile([P, 6 * len(STAT_PARTS)], F32, tag="stats", name="stats")
            nc.vector.bn_stats(
                out=tiles["stats", m][:, part * 6 : (part + 1) * 6],
                in_=tiles["y", m][:, STAT_PARTS[part][0] * DH : STAT_PARTS[part][1] * DH],
            )

        def aggregate(m):
            mv = small.tile([P, 2], F32, tag="mv", name="mv")
            nc.vector.bn_aggr(out=mv[:], in_=tiles["stats", m][:])
            tiles["mean", m] = mv
            deviation = small.tile([P, 1], F32, tag="deviation", name="deviation")
            nc.scalar.activation(out=deviation[:], in_=mv[:, 1:2], func=ACT.Sqrt, bias=LN_EPS, scale=1.0)
            tiles["deviation", m] = deviation

        def invert(m):
            rstd = small.tile([P, 1], F32, tag="rstd", name="rstd")
            nc.vector.reciprocal(out=rstd[:], in_=tiles["deviation", m][:])
            tiles["rstd", m] = rstd

        def warm_sqrt():
            nc.scalar.activation(out=warm[:], in_=warm[:], func=ACT.Sqrt)

        halves = (slice(0, 512), slice(512, 1024))
        QUARTERS = tuple(slice(c, c + 256) for c in range(0, D, 256))

        def store(m, cols, queue=nc.sync):
            rows = tokens(out[m // TT])[:, m % TT, :]
            queue.dma_start(out=rows[:, cols], in_=tiles["res", m][:, cols])

        def normalise_gpsimd(m, parts):
            if ("res", m) not in tiles:
                tiles["res", m] = y_pool.tile([P, D], F32, tag="res", name="res")
            res = tiles["res", m]
            for cols in parts:
                nc.gpsimd.tensor_scalar(
                    out=res[:, cols],
                    in0=tiles["y", m][:, cols],
                    scalar1=tiles["negmu", m][:],
                    scalar2=tiles["rstd", m][:],
                    op0=ALU.add,
                    op1=ALU.mult,
                )
            for cols in parts:
                nc.gpsimd.tensor_tensor(
                    out=res[:, cols], in0=res[:, cols], in1=gamma_b[:, cols], op=ALU.mult
                )
            for cols in parts:
                nc.gpsimd.tensor_tensor(
                    out=res[:, cols], in0=res[:, cols], in1=beta_b[:, cols], op=ALU.add
                )
                if m < UNITS - VECTOR_UNITS:
                    store(m, cols)

        def center(m, parts):
            if ("res", m) not in tiles:
                tiles["res", m] = y_pool.tile([P, D], F32, tag="res", name="res")
            res = tiles["res", m]
            aggregated = ("mean", m) in tiles
            for cols in parts:
                nc.vector.scalar_tensor_tensor(
                    out=res[:, cols],
                    in0=tiles["y", m][:, cols],
                    scalar=tiles["mean", m][:, 0:1] if aggregated else tiles["negmu", m][:],
                    in1=gamma_b[:, cols],
                    op0=ALU.subtract if aggregated else ALU.add,
                    op1=ALU.mult,
                )

        def scale(m, parts):
            for cols in parts:
                nc.vector.scalar_tensor_tensor(
                    out=tiles["res", m][:, cols],
                    in0=tiles["res", m][:, cols],
                    scalar=tiles["rstd", m][:],
                    in1=beta_b[:, cols],
                    op0=ALU.mult,
                    op1=ALU.add,
                )
                store(m, cols)

        def ev_step(n):
            return max(2 * n + 3, EV_FIRST + n) if n < HALVES // 2 else max(2 * n + 3, EV_SECOND + n - HALVES // 2)

        plan = {}
        among = {}

        def at(step, call, *args):
            plan.setdefault(step, []).append((call, args))

        last = UNITS - 1
        for n in range(HALVES):
            among[2 * n + RECIP] = [(reciprocals, (n,))]
            at(max(2 * n + MASKED, ev_step(n) - R_EARLY), masked_reciprocals, n)
        for n in range(HALVES):
            if n == HALVES - 1:
                for i, pair in enumerate(((0, 1), (2, 3))):
                    at(2 * n + 2 + i, quantise_e, n, pair)
                    at(2 * n + 2 + i, e_times_v, n, pair)
                for i, pair in enumerate(((0, 1), (2, 3))):
                    at(2 * n + 3 + i, residual, n, pair)
                continue
            at(2 * n + 3, quantise_e, n)
            at(ev_step(n), e_times_v, n)
            at(ev_step(n) + 1, residual, n)
        for m in range(UNITS):
            s = ev_step(2 * m + 1) + 2
            if m < UNITS - VECTOR_UNITS:
                at(s, mean, m)
                at(s, row_statistics, m)
                at(s + 1, normalise_gpsimd, m, halves)
            elif m < last:
                at(s, mean, m)
                at(s + 1, row_statistics, m)
                at(s + CENTER, center, m, halves[:1])
                at(s + 2, normalise_gpsimd, m, halves[1:])
                at(s + 4, scale, m, halves[:1])
            else:
                at(s - 2, part_statistics, m, 0)
                at(s - 2, part_statistics, m, 1)
                at(s - 1, part_statistics, m, 2)
                at(s - 1, warm_sqrt)
                at(s - 1, aggregate, m)
                at(s, center, m, halves)
                at(s, invert, m)
                at(s, store, m - 1, halves[1], nc.scalar)
                at(s + 1, scale, m, QUARTERS)
        for j in range(AHEAD):
            scores(j)
            row_max(j)
        scores(AHEAD)
        for step in range(max(plan) + 1):
            if 0 <= step - 1 < PAIRS:
                transpose_e(step - 1)
            if step + AHEAD + 1 < PAIRS:
                scores(step + AHEAD + 1)
            if step + AHEAD < PAIRS:
                row_max(step + AHEAD, among.get(step, []))
            else:
                for call, args in among.get(step, []):
                    call(*args)
            if step < PAIRS:
                exponentials(step)
            if 0 <= step - 1 < PAIRS:
                copy_e(step - 1)
            for call, args in plan.get(step, []):
                call(*args)
            for i in range(JOBS_FIRST if step < EV_FIRST else JOBS_PER_STEP):
                advance()
